import numpy as np
import ml_dtypes


def mxq(x, axis, fmt="e4m3"):
    dtype, down = {"e4m3": (ml_dtypes.float8_e4m3fn, 7), "e5m2": (ml_dtypes.float8_e5m2, 14)}[fmt]
    v = np.moveaxis(np.asarray(x, np.float32).astype(ml_dtypes.bfloat16).astype(np.float64), axis, -1)
    blocks = v.reshape(v.shape[:-1] + (-1, 32))
    amax = np.abs(blocks).max(-1, keepdims=True)
    byte = np.maximum(np.where(amax > 0, np.frexp(amax)[1] - 1 + 127, 0) - down, 1)
    scale = np.exp2(byte - 127.0)
    codes = (blocks / scale).astype(np.float32).astype(dtype).astype(np.float64)
    return np.moveaxis((codes * scale).reshape(v.shape), -1, axis)


WIDE = False


def mx_kscale(k):
    if not WIDE:
        return np.ones(k)
    levels = np.array([10, -10, 5, -5, 0])
    if k % 512:
        return np.exp2(np.random.permutation(np.resize(levels, k // 32))).repeat(32)
    a = np.empty((k // 512, 16))
    for p in range(k // 512):
        a[p, :8] = np.random.permutation(np.resize(levels, 8))
        for g in range(8):
            far = levels[np.abs(levels - a[p, g]) >= 10]
            a[p, g + 8] = far[np.random.randint(len(far))]
    return np.exp2(a.ravel()).repeat(32)


BF16 = ml_dtypes.bfloat16


def bf(x):
    return np.asarray(x, np.float32).astype(BF16)


def f64(x):
    return np.asarray(x).astype(np.float64)


B, S, H, E, D, TRAIN_LEN = 1, 1024, 1024, 1536, 128, 512


def silu(v):
    return v / (1.0 + np.exp(-v))


def apply_rotary(x, sin, cos):
    x1, x2 = x[..., 0::2], x[..., 1::2]
    return np.concatenate([x1 * cos - x2 * sin, x1 * sin + x2 * cos], axis=-1)


def draw0():
    s = mx_kscale(H)
    pos = np.arange(S)[:, None]
    inv = np.exp(-np.arange(0, D, 2) / D * np.log(10000.0))
    ang = pos * inv[None, :]
    return {"hidden_states": bf(np.random.standard_normal((B, S, H)) * s),
            "sin": bf(np.sin(ang)[None]),
            "cos": bf(np.cos(ang)[None]),
            "W_i": bf(np.random.standard_normal((H, 2 * E + D)) / np.sqrt(H) / s[:, None]),
            "q_scale": bf(1.0 + 0.1 * np.random.standard_normal(D)),
            "k_scale": bf(1.0 + 0.1 * np.random.standard_normal(D))}


def core(hidden_states, sin, cos, W_i, q_scale, k_scale):
    x = silu(mxq(f64(hidden_states), 2, "e4m3") @ mxq(f64(W_i), 0, "e4m3"))
    u, v, qk = np.split(x, [E, 2 * E], axis=-1)
    sn, cs = f64(sin), f64(cos)
    q = apply_rotary(qk * f64(q_scale), sn, cs)
    k = apply_rotary(qk * f64(k_scale), sn, cs)
    return u, v, q, k


def e4m3fn_bytes(y):
    return np.clip(np.asarray(y, np.float64), -448.0, 448.0).astype(np.float32).astype(ml_dtypes.float8_e4m3fn).view(np.uint8)


def e4m3fn_values(b):
    return np.asarray(b, np.uint8).view(ml_dtypes.float8_e4m3fn).astype(np.float64)


def setup_inputs():
    d = draw0()
    x0 = np.asarray(d['W_i']).astype(np.float64)
    s = (np.max(np.abs(x0), axis=(1,), keepdims=True) / 448.0).astype(np.float32)
    out = {}
    for k, v in d.items():
        if k == 'W_i':
            out['W_i_bytes'] = e4m3fn_bytes(x0 / s.astype(np.float64))
            out['W_i_scale'] = s
        else:
            out[k] = v
    return out


def reference(hidden_states, sin, cos, W_i_bytes, W_i_scale, q_scale, k_scale):
    return core(hidden_states, sin, cos, e4m3fn_values(W_i_bytes) * W_i_scale.astype(np.float64), q_scale, k_scale)

@@ -1,0 +1,245 @@
+from contextlib import ExitStack
+
+import concourse.mybir as mybir
+from concourse.masks import make_identity
+
+TOKENS, HIDDEN, EXPAND, HEAD = 1024, 1024, 1536, 128
+COLUMNS = 2 * EXPAND + HEAD
+FLOPS = 2 * TOKENS * HIDDEN * COLUMNS
+
+F32 = mybir.dt.float32
+BF16 = mybir.dt.bfloat16
+U32 = mybir.dt.uint32
+U8 = mybir.dt.uint8
+FP8 = mybir.dt.float8_e4m3fn
+FP8X4 = mybir.dt.float8_e4m3fn_x4
+ACT = mybir.ActivationFunctionType
+ALU = mybir.AluOpType
+
+P = 128
+PACK = 4
+PASSES = HIDDEN // (P * PACK)
+TOKEN_TILES = TOKENS // P
+HALF = HEAD // 2
+
+CHUNKS = (
+    (0, 512, 0),
+    (512, 512, 0),
+    (1024, 512, 0),
+    (3072, 128, 2),
+    (1536, 512, 1),
+    (2048, 512, 1),
+    (2560, 512, 1),
+)
+LOADS = ((0, 512), (512, 1536), (1536, 3200))
+SCALAR_UNITS = ()
+SCALAR_PLANES = (0, 0, 1, 2, 1, 2, 0, 0, 1, 2, 1, 2, 1, 1)
+LAG = 2
+
+
+def tile_gatedattentionunit_pa_kernel(
+    tc, hidden_states, sin, cos, W_i_bytes, W_i_scale, q_scale, k_scale, out_0, out_1, out_2, out_3
+):
+    nc = tc.nc
+    with ExitStack() as ctx:
+        const = ctx.enter_context(tc.tile_pool(name="const", bufs=1))
+        keep = ctx.enter_context(tc.tile_pool(name="keep", bufs=1))
+        stage = ctx.enter_context(tc.tile_pool(name="stage", bufs=3))
+        outp = ctx.enter_context(tc.tile_pool(name="outp", bufs=6))
+        rope = ctx.enter_context(tc.tile_pool(name="rope", bufs=1))
+        psum = ctx.enter_context(tc.psum_pool(name="psum", bufs=2))
+
+        w_scale = const.tile([P, PASSES, PACK], F32, name="w_scale")
+        nc.scalar.dma_start(
+            out=w_scale[:], in_=W_i_scale.rearrange("(g p t) o -> p g (t o)", p=P, t=PACK)
+        )
+        warm = const.tile([P, 2], F32, name="warm")
+        nc.vector.memset(warm[:, 0:1], 0.0)
+        nc.scalar.activation(out=warm[:, 1:2], in_=warm[:, 0:1], func=ACT.Silu)
+        ident = const.tile([P, P], F32, name="ident")
+        make_identity(nc, ident[:])
+
+        x_view = hidden_states.rearrange("o (m p) k -> (o m) p k", p=P)
+        w_view = W_i_bytes.rearrange("(g p t) n -> g p t n", p=P, t=PACK)
+        x_sb = [keep.tile([P, HIDDEN], BF16, name="x_sb%d" % m) for m in range(TOKEN_TILES)]
+        w_bytes = [
+            [keep.tile([P, PACK, c1 - c0], U8, name="w_bytes%d_%d" % (i, g)) for g in range(PASSES)]
+            for i, (c0, c1) in enumerate(LOADS)
+        ]
+
+        def load_x(m):
+            nc.sync.dma_start(out=x_sb[m][:], in_=x_view[m])
+
+        def load_w(i, g):
+            c0, c1 = LOADS[i]
+            nc.sync.dma_start(out=w_bytes[i][g][:], in_=w_view[g][:, :, c0:c1])
+
+        load_w(0, 0)
+        load_w(0, 1)
+        load_x(0)
+        load_x(1)
+        load_w(1, 0)
+        load_x(2)
+        load_x(3)
+        load_x(4)
+        load_w(1, 1)
+        load_x(5)
+        load_x(6)
+        load_x(7)
+        load_w(2, 0)
+        load_w(2, 1)
+        cos_sb = const.tile([P, TOKEN_TILES, HALF], BF16, name="cos_sb")
+        sin_sb = const.tile([P, TOKEN_TILES, HALF], BF16, name="sin_sb")
+        gains = const.tile([P, 2, HEAD], BF16, name="gains")
+        nc.sync.dma_start(out=cos_sb[:], in_=cos.rearrange("o (m p) i -> p (o m) i", p=P))
+        nc.sync.dma_start(out=sin_sb[:], in_=sin.rearrange("o (m p) i -> p (o m) i", p=P))
+        nc.sync.dma_start(out=gains[:, 0, :], in_=q_scale.partition_broadcast(P))
+        nc.sync.dma_start(out=gains[:, 1, :], in_=k_scale.partition_broadcast(P))
+
+        x_codes = [keep.tile([P, PASSES * P], U32, name="x_codes%d" % m, align_bytes=64) for m in range(TOKEN_TILES)]
+        x_scales = [keep.tile([P, PASSES * P], U8, name="x_scales%d" % m, align_bytes=64) for m in range(TOKEN_TILES)]
+        x_grouped = {}
+
+        def turn_x(m):
+            words = x_sb[m][:].bitcast(F32)
+            xt = psum.tile([P, PASSES, 2, P], F32, tag="xt", bufs=2)
+            for g in range(PASSES):
+                for u in range(2):
+                    nc.tensor.transpose(
+                        xt[:, g, u, :], words[:, 256 * g + u : 256 * (g + 1) : 2], ident[:]
+                    )
+            grouped = stage.tile([P, PASSES, P, PACK], BF16, tag="x_grouped", bufs=8, align_bytes=64)
+            nc.scalar.copy(out=grouped[:].bitcast(F32), in_=xt[:].rearrange("p g u r -> p g r u"))
+            x_grouped[m] = grouped
+
+        def quantise_x(m):
+            nc.vector.quantize_mx(
+                out=x_codes[m][:].bitcast(FP8X4),
+                scales=x_scales[m][:],
+                in_=x_grouped[m][:].rearrange("p g r t -> p (g r t)"),
+            )
+
+        w_codes = [keep.tile([P, PASSES * w], U32, name="w_codes%d" % j, align_bytes=64) for j, (c, w, o) in enumerate(CHUNKS)]
+        w_scales = [keep.tile([P, PASSES * w], U8, name="w_scales%d" % j, align_bytes=64) for j, (c, w, o) in enumerate(CHUNKS)]
+        units = [(j, g) for j in range(len(CHUNKS)) for g in range(PASSES)]
+        w_planes = {}
+        w_grouped = {}
+
+        def widen(i):
+            j, g = units[i]
+            c, w, o = CHUNKS[j]
+            li = [n for n, (c0, c1) in enumerate(LOADS) if c0 <= c and c + w <= c1][0]
+            off = c - LOADS[li][0]
+            planes = stage.tile([P, PACK, w], BF16, tag="w_planes", bufs=4, align_bytes=64)
+            for t in range(PACK):
+                codes = w_bytes[li][g][:, t, off : off + w].bitcast(FP8)
+                if t >= PACK - SCALAR_PLANES[i]:
+                    nc.scalar.activation(
+                        out=planes[:, t, :], in_=codes, func=ACT.Copy, scale=w_scale[:, g, t : t + 1]
+                    )
+                else:
+                    nc.vector.tensor_scalar(
+                        out=planes[:, t, :],
+                        in0=codes,
+                        scalar1=w_scale[:, g, t : t + 1],
+                        scalar2=None,
+                        op0=ALU.mult,
+                    )
+            w_planes[i] = planes
+
+        def interleave(i):
+            j, g = units[i]
+            c, w, o = CHUNKS[j]
+            grouped = stage.tile([P, w, PACK], BF16, tag="w_grouped", bufs=3, align_bytes=64)
+            src = w_planes[i][:].rearrange("p t c -> p c t")
+            if i in SCALAR_UNITS:
+                nc.scalar.copy(out=grouped[:], in_=src)
+            else:
+                nc.vector.tensor_copy(out=grouped[:], in_=src)
+            w_grouped[i] = grouped
+
+        def quantise_w(i):
+            j, g = units[i]
+            c, w, o = CHUNKS[j]
+            nc.vector.quantize_mx(
+                out=w_codes[j][:, g * w : (g + 1) * w].bitcast(FP8X4),
+                scales=w_scales[j][:, g * w : (g + 1) * w],
+                in_=w_grouped[i][:].rearrange("p c t -> p (c t)"),
+            )
+
+        qk_act = rope.tile([P, TOKEN_TILES, HEAD], F32, name="qk_act")
+
+        def product(acc, j, m):
+            c, w, o = CHUNKS[j]
+            for g in range(PASSES):
+                nc.tensor.matmul_mx(
+                    out=acc,
+                    lhsT=x_codes[m][:, g * P : (g + 1) * P].bitcast(FP8X4),
+                    lhsT_scale=x_scales[m][:, g * P : (g + 1) * P],
+                    rhs=w_codes[j][:, g * w : (g + 1) * w].bitcast(FP8X4),
+                    rhs_scale=w_scales[j][:, g * w : (g + 1) * w],
+                    start=(g == 0),
+                    stop=(g == PASSES - 1),
+                )
+
+        def chunk(j):
+            c, w, o = CHUNKS[j]
+            if o == 2:
+                for h in range(TOKEN_TILES // 4):
+                    acc = psum.tile([P, 4, HEAD], F32, tag="acc", bufs=6)
+                    for r in range(4):
+                        product(acc[:, r, :], j, 4 * h + r)
+                    nc.scalar.activation(out=qk_act[:, 4 * h : 4 * h + 4, :], in_=acc[:], func=ACT.Silu)
+                return
+            dst = (out_0, out_1)[o]
+            d0 = c - o * EXPAND
+            for m in range(TOKEN_TILES):
+                acc = psum.tile([P, w], F32, tag="acc", bufs=6)
+                product(acc[:], j, m)
+                res = outp.tile([P, w], F32, tag="res")
+                nc.scalar.activation(out=res[:], in_=acc[:], func=ACT.Silu)
+                nc.sync.dma_start(out=dst[0, m * P : (m + 1) * P, d0 : d0 + w], in_=res[:])
+
+        def rotate(a, dst):
+            y = rope.tile([P, TOKEN_TILES, HEAD], F32, tag="y")
+            nc.vector.tensor_tensor(
+                out=y[:],
+                in0=qk_act[:],
+                in1=gains[:, a, :].unsqueeze(1).to_broadcast([P, TOKEN_TILES, HEAD]),
+                op=ALU.mult,
+            )
+            pairs = y[:].rearrange("p m (i e) -> p m i e", e=2)
+            y1 = pairs[:, :, :, 0]
+            y2 = pairs[:, :, :, 1]
+            t1 = rope.tile([P, TOKEN_TILES, HALF], F32, tag="t1")
+            t2 = rope.tile([P, TOKEN_TILES, HALF], F32, tag="t2")
+            t3 = rope.tile([P, TOKEN_TILES, HALF], F32, tag="t3")
+            t4 = rope.tile([P, TOKEN_TILES, HALF], F32, tag="t4")
+            res = rope.tile([P, TOKEN_TILES, HEAD], F32, tag="rot", bufs=2)
+            nc.vector.tensor_tensor(out=t1[:], in0=y1, in1=cos_sb[:], op=ALU.mult)
+            nc.vector.tensor_tensor(out=t2[:], in0=y2, in1=sin_sb[:], op=ALU.mult)
+            nc.vector.tensor_tensor(out=t3[:], in0=y1, in1=sin_sb[:], op=ALU.mult)
+            nc.vector.tensor_tensor(out=t4[:], in0=y2, in1=cos_sb[:], op=ALU.mult)
+            nc.vector.tensor_tensor(out=res[:, :, 0:HALF], in0=t1[:], in1=t2[:], op=ALU.subtract)
+            nc.vector.tensor_tensor(out=res[:, :, HALF:HEAD], in0=t3[:], in1=t4[:], op=ALU.add)
+            nc.sync.dma_start(out=dst.rearrange("o (m p) c -> p (o m) c", p=P), in_=res[:])
+
+        for m in range(TOKEN_TILES):
+            turn_x(m)
+        widen(0)
+        for i in range(len(units)):
+            interleave(i)
+            if i + 1 < len(units):
+                widen(i + 1)
+            quantise_w(i)
+            if i == 0:
+                for m in range(3):
+                    quantise_x(m)
+            if i == 1:
+                for m in range(3, TOKEN_TILES):
+                    quantise_x(m)
+            if i >= LAG and units[i - LAG][1] == PASSES - 1:
+                chunk(units[i - LAG][0])
+        chunk(len(CHUNKS) - 1)
+        rotate(0, out_2)
+        rotate(1, out_3)

@@ -21,20 +21,11 @@ PACK = 4
 PASSES = HIDDEN // (P * PACK)
 TOKEN_TILES = TOKENS // P
 HALF = HEAD // 2
+N_TILE = 512
 
-CHUNKS = (
-    (0, 512, 0),
-    (512, 512, 0),
-    (1024, 512, 0),
-    (3072, 128, 2),
-    (1536, 512, 1),
-    (2048, 512, 1),
-    (2560, 512, 1),
-)
-LOADS = ((0, 512), (512, 1536), (1536, 3200))
-SCALAR_UNITS = ()
-SCALAR_PLANES = (0, 0, 1, 2, 1, 2, 0, 0, 1, 2, 1, 2, 1, 1)
-LAG = 2
+GROUPS = ((0, 512), (2560, 640), (512, 1024), (1536, 1024))
+SCALAR_PLANES = ((0, 0), (1, 1), (1, 2), (1, 2))
+RES_BUFS = 16
 
 
 def tile_gatedattentionunit_pa_kernel(
@@ -44,8 +35,8 @@ def tile_gatedattentionunit_pa_kernel(
     with ExitStack() as ctx:
         const = ctx.enter_context(tc.tile_pool(name="const", bufs=1))
         keep = ctx.enter_context(tc.tile_pool(name="keep", bufs=1))
-        stage = ctx.enter_context(tc.tile_pool(name="stage", bufs=3))
-        outp = ctx.enter_context(tc.tile_pool(name="outp", bufs=6))
+        stage = ctx.enter_context(tc.tile_pool(name="stage", bufs=4))
+        outp = ctx.enter_context(tc.tile_pool(name="outp", bufs=RES_BUFS))
         rope = ctx.enter_context(tc.tile_pool(name="rope", bufs=1))
         psum = ctx.enter_context(tc.psum_pool(name="psum", bufs=2))
 
@@ -53,193 +44,193 @@ def tile_gatedattentionunit_pa_kernel(
         nc.scalar.dma_start(
             out=w_scale[:], in_=W_i_scale.rearrange("(g p t) o -> p g (t o)", p=P, t=PACK)
         )
+        gain_row = const.tile([P, 2, HEAD], BF16, name="gain_row")
+        nc.gpsimd.memset(gain_row[:], 0.0)
+        nc.scalar.dma_start(out=gain_row[0:1, 0, :], in_=q_scale.unsqueeze(0))
+        nc.scalar.dma_start(out=gain_row[0:1, 1, :], in_=k_scale.unsqueeze(0))
         warm = const.tile([P, 2], F32, name="warm")
         nc.vector.memset(warm[:, 0:1], 0.0)
         nc.scalar.activation(out=warm[:, 1:2], in_=warm[:, 0:1], func=ACT.Silu)
+        ones = const.tile([P, P], BF16, name="ones")
+        nc.vector.memset(ones[:], 1.0)
         ident = const.tile([P, P], F32, name="ident")
         make_identity(nc, ident[:])
 
-        x_view = hidden_states.rearrange("o (m p) k -> (o m) p k", p=P)
+        x_view = hidden_states.rearrange("o (p m) k -> p (o m) k", m=TOKEN_TILES)
         w_view = W_i_bytes.rearrange("(g p t) n -> g p t n", p=P, t=PACK)
-        x_sb = [keep.tile([P, HIDDEN], BF16, name="x_sb%d" % m) for m in range(TOKEN_TILES)]
+        x_sb = [keep.tile([P, 2, HIDDEN], BF16, name="x_sb%d" % h) for h in range(TOKEN_TILES // 2)]
         w_bytes = [
-            [keep.tile([P, PACK, c1 - c0], U8, name="w_bytes%d_%d" % (i, g)) for g in range(PASSES)]
-            for i, (c0, c1) in enumerate(LOADS)
+            [keep.tile([P, PACK, width], U8, name="w_bytes%d_%d" % (n, g)) for g in range(PASSES)]
+            for n, (c0, width) in enumerate(GROUPS)
         ]
 
-        def load_x(m):
-            nc.sync.dma_start(out=x_sb[m][:], in_=x_view[m])
+        def load_w(n):
+            c0, width = GROUPS[n]
+            for g in range(PASSES):
+                nc.sync.dma_start(out=w_bytes[n][g][:], in_=w_view[g][:, :, c0 : c0 + width])
 
-        def load_w(i, g):
-            c0, c1 = LOADS[i]
-            nc.sync.dma_start(out=w_bytes[i][g][:], in_=w_view[g][:, :, c0:c1])
-
-        load_w(0, 0)
-        load_w(0, 1)
-        load_x(0)
-        load_x(1)
-        load_w(1, 0)
-        load_x(2)
-        load_x(3)
-        load_x(4)
-        load_w(1, 1)
-        load_x(5)
-        load_x(6)
-        load_x(7)
-        load_w(2, 0)
-        load_w(2, 1)
+        load_w(0)
+        for h in range(TOKEN_TILES // 2):
+            nc.sync.dma_start(out=x_sb[h][:], in_=x_view[:, 2 * h : 2 * h + 2, :])
+        for n in range(1, len(GROUPS)):
+            load_w(n)
         cos_sb = const.tile([P, TOKEN_TILES, HALF], BF16, name="cos_sb")
         sin_sb = const.tile([P, TOKEN_TILES, HALF], BF16, name="sin_sb")
-        gains = const.tile([P, 2, HEAD], BF16, name="gains")
-        nc.sync.dma_start(out=cos_sb[:], in_=cos.rearrange("o (m p) i -> p (o m) i", p=P))
-        nc.sync.dma_start(out=sin_sb[:], in_=sin.rearrange("o (m p) i -> p (o m) i", p=P))
-        nc.sync.dma_start(out=gains[:, 0, :], in_=q_scale.partition_broadcast(P))
-        nc.sync.dma_start(out=gains[:, 1, :], in_=k_scale.partition_broadcast(P))
+        nc.sync.dma_start(out=cos_sb[:], in_=cos.rearrange("o (p m) i -> p (o m) i", m=TOKEN_TILES))
+        nc.sync.dma_start(out=sin_sb[:], in_=sin.rearrange("o (p m) i -> p (o m) i", m=TOKEN_TILES))
 
-        x_codes = [keep.tile([P, PASSES * P], U32, name="x_codes%d" % m, align_bytes=64) for m in range(TOKEN_TILES)]
-        x_scales = [keep.tile([P, PASSES * P], U8, name="x_scales%d" % m, align_bytes=64) for m in range(TOKEN_TILES)]
+        gain_ps = psum.tile([P, 2, HEAD], F32, tag="acc", bufs=6)
+        nc.tensor.matmul(
+            out=gain_ps[:].rearrange("p a c -> p (a c)"),
+            lhsT=ones[:],
+            rhs=gain_row[:].rearrange("p a c -> p (a c)"),
+            start=True,
+            stop=True,
+        )
+        gains = const.tile([P, 2, HEAD], F32, name="gains")
+        nc.scalar.copy(out=gains[:], in_=gain_ps[:])
+
+        x_codes = [keep.tile([P, 2 * PASSES * P], U32, name="x_codes%d" % h, align_bytes=64) for h in range(TOKEN_TILES // 2)]
+        x_scales = [keep.tile([P, 2 * PASSES * P], U8, name="x_scales%d" % h, align_bytes=64) for h in range(TOKEN_TILES // 2)]
         x_grouped = {}
 
         def turn_x(m):
-            words = x_sb[m][:].bitcast(F32)
+            h, a = divmod(m, 2)
+            words = x_sb[h][:, a, :].bitcast(F32)
             xt = psum.tile([P, PASSES, 2, P], F32, tag="xt", bufs=2)
             for g in range(PASSES):
                 for u in range(2):
                     nc.tensor.transpose(
                         xt[:, g, u, :], words[:, 256 * g + u : 256 * (g + 1) : 2], ident[:]
                     )
-            grouped = stage.tile([P, PASSES, P, PACK], BF16, tag="x_grouped", bufs=8, align_bytes=64)
-            nc.scalar.copy(out=grouped[:].bitcast(F32), in_=xt[:].rearrange("p g u r -> p g r u"))
-            x_grouped[m] = grouped
-
-        def quantise_x(m):
-            nc.vector.quantize_mx(
-                out=x_codes[m][:].bitcast(FP8X4),
-                scales=x_scales[m][:],
-                in_=x_grouped[m][:].rearrange("p g r t -> p (g r t)"),
+            if a == 0:
+                x_grouped[h] = stage.tile([P, 2, PASSES, P, PACK], BF16, tag="x_grouped", bufs=4, align_bytes=64, name="x_grouped")
+            nc.scalar.copy(
+                out=x_grouped[h][:, a].bitcast(F32), in_=xt[:].rearrange("p g u r -> p g r u")
             )
 
-        w_codes = [keep.tile([P, PASSES * w], U32, name="w_codes%d" % j, align_bytes=64) for j, (c, w, o) in enumerate(CHUNKS)]
-        w_scales = [keep.tile([P, PASSES * w], U8, name="w_scales%d" % j, align_bytes=64) for j, (c, w, o) in enumerate(CHUNKS)]
-        units = [(j, g) for j in range(len(CHUNKS)) for g in range(PASSES)]
+        def quantise_x(h):
+            nc.vector.quantize_mx(
+                out=x_codes[h][:].bitcast(FP8X4),
+                scales=x_scales[h][:],
+                in_=x_grouped[h][:].rearrange("p a g r t -> p (a g r t)"),
+            )
+
         w_planes = {}
-        w_grouped = {}
 
-        def widen(i):
-            j, g = units[i]
-            c, w, o = CHUNKS[j]
-            li = [n for n, (c0, c1) in enumerate(LOADS) if c0 <= c and c + w <= c1][0]
-            off = c - LOADS[li][0]
-            planes = stage.tile([P, PACK, w], BF16, tag="w_planes", bufs=4, align_bytes=64)
-            for t in range(PACK):
-                codes = w_bytes[li][g][:, t, off : off + w].bitcast(FP8)
-                if t >= PACK - SCALAR_PLANES[i]:
-                    nc.scalar.activation(
-                        out=planes[:, t, :], in_=codes, func=ACT.Copy, scale=w_scale[:, g, t : t + 1]
-                    )
-                else:
-                    nc.vector.tensor_scalar(
-                        out=planes[:, t, :],
-                        in0=codes,
-                        scalar1=w_scale[:, g, t : t + 1],
-                        scalar2=None,
-                        op0=ALU.mult,
-                    )
-            w_planes[i] = planes
+        def widen(n, scalar_share):
+            c0, width = GROUPS[n]
+            for g in range(PASSES):
+                if (n, g) not in w_planes:
+                    w_planes[(n, g)] = stage.tile([P, PACK, width], BF16, tag="w_planes", bufs=4, align_bytes=64, name="w_planes")
+                planes = w_planes[(n, g)]
+                for t in range(PACK):
+                    codes = w_bytes[n][g][:, t, :].bitcast(FP8)
+                    on_scalar = t >= PACK - SCALAR_PLANES[n][g]
+                    if on_scalar and scalar_share:
+                        nc.scalar.activation(
+                            out=planes[:, t, :], in_=codes, func=ACT.Copy, scale=w_scale[:, g, t : t + 1]
+                        )
+                    if not on_scalar and not scalar_share:
+                        nc.vector.tensor_scalar(
+                            out=planes[:, t, :],
+                            in0=codes,
+                            scalar1=w_scale[:, g, t : t + 1],
+                            scalar2=None,
+                            op0=ALU.mult,
+                        )
 
-        def interleave(i):
-            j, g = units[i]
-            c, w, o = CHUNKS[j]
-            grouped = stage.tile([P, w, PACK], BF16, tag="w_grouped", bufs=3, align_bytes=64)
-            src = w_planes[i][:].rearrange("p t c -> p c t")
-            if i in SCALAR_UNITS:
-                nc.scalar.copy(out=grouped[:], in_=src)
-            else:
-                nc.vector.tensor_copy(out=grouped[:], in_=src)
-            w_grouped[i] = grouped
-
-        def quantise_w(i):
-            j, g = units[i]
-            c, w, o = CHUNKS[j]
-            nc.vector.quantize_mx(
-                out=w_codes[j][:, g * w : (g + 1) * w].bitcast(FP8X4),
-                scales=w_scales[j][:, g * w : (g + 1) * w],
-                in_=w_grouped[i][:].rearrange("p c t -> p (c t)"),
-            )
+        def quantise_w(n, off, w):
+            codes = keep.tile([P, PASSES * w], U32, name="w_codes%d_%d" % (n, off), align_bytes=64)
+            scales = keep.tile([P, PASSES * w], U8, name="w_scales%d_%d" % (n, off), align_bytes=64)
+            grouped = []
+            for g in range(PASSES):
+                gr = stage.tile([P, w, PACK], BF16, tag="w_grouped", bufs=4, align_bytes=64)
+                nc.vector.tensor_copy(
+                    out=gr[:], in_=w_planes[(n, g)][:, :, off : off + w].rearrange("p t c -> p c t")
+                )
+                grouped.append(gr)
+            for g in range(PASSES):
+                nc.vector.quantize_mx(
+                    out=codes[:, g * w : (g + 1) * w].bitcast(FP8X4),
+                    scales=scales[:, g * w : (g + 1) * w],
+                    in_=grouped[g][:].rearrange("p c t -> p (c t)"),
+                )
+            return codes, scales
 
         qk_act = rope.tile([P, TOKEN_TILES, HEAD], F32, name="qk_act")
+        out_views = [o.rearrange("o (p m) c -> (o m) p c", m=TOKEN_TILES) for o in (out_0, out_1)]
 
-        def product(acc, j, m):
-            c, w, o = CHUNKS[j]
+        def product(acc, codes, scales, w, m):
+            h, a = divmod(m, 2)
             for g in range(PASSES):
+                x0 = (a * PASSES + g) * P
                 nc.tensor.matmul_mx(
                     out=acc,
-                    lhsT=x_codes[m][:, g * P : (g + 1) * P].bitcast(FP8X4),
-                    lhsT_scale=x_scales[m][:, g * P : (g + 1) * P],
-                    rhs=w_codes[j][:, g * w : (g + 1) * w].bitcast(FP8X4),
-                    rhs_scale=w_scales[j][:, g * w : (g + 1) * w],
+                    lhsT=x_codes[h][:, x0 : x0 + P].bitcast(FP8X4),
+                    lhsT_scale=x_scales[h][:, x0 : x0 + P],
+                    rhs=codes[:, g * w : (g + 1) * w].bitcast(FP8X4),
+                    rhs_scale=scales[:, g * w : (g + 1) * w],
                     start=(g == 0),
                     stop=(g == PASSES - 1),
                 )
 
-        def chunk(j):
-            c, w, o = CHUNKS[j]
-            if o == 2:
+        def chunk(c, w, codes, scales):
+            if c >= 2 * EXPAND:
                 for h in range(TOKEN_TILES // 4):
                     acc = psum.tile([P, 4, HEAD], F32, tag="acc", bufs=6)
                     for r in range(4):
-                        product(acc[:, r, :], j, 4 * h + r)
+                        product(acc[:, r, :], codes, scales, w, 4 * h + r)
                     nc.scalar.activation(out=qk_act[:, 4 * h : 4 * h + 4, :], in_=acc[:], func=ACT.Silu)
                 return
-            dst = (out_0, out_1)[o]
-            d0 = c - o * EXPAND
+            o, d0 = divmod(c, EXPAND)
             for m in range(TOKEN_TILES):
                 acc = psum.tile([P, w], F32, tag="acc", bufs=6)
-                product(acc[:], j, m)
+                product(acc[:], codes, scales, w, m)
                 res = outp.tile([P, w], F32, tag="res")
                 nc.scalar.activation(out=res[:], in_=acc[:], func=ACT.Silu)
-                nc.sync.dma_start(out=dst[0, m * P : (m + 1) * P, d0 : d0 + w], in_=res[:])
+                nc.sync.dma_start(out=out_views[o][m][:, d0 : d0 + w], in_=res[:])
 
-        def rotate(a, dst):
-            y = rope.tile([P, TOKEN_TILES, HEAD], F32, tag="y")
-            nc.vector.tensor_tensor(
-                out=y[:],
-                in0=qk_act[:],
-                in1=gains[:, a, :].unsqueeze(1).to_broadcast([P, TOKEN_TILES, HEAD]),
-                op=ALU.mult,
-            )
-            pairs = y[:].rearrange("p m (i e) -> p m i e", e=2)
-            y1 = pairs[:, :, :, 0]
-            y2 = pairs[:, :, :, 1]
-            t1 = rope.tile([P, TOKEN_TILES, HALF], F32, tag="t1")
-            t2 = rope.tile([P, TOKEN_TILES, HALF], F32, tag="t2")
-            t3 = rope.tile([P, TOKEN_TILES, HALF], F32, tag="t3")
-            t4 = rope.tile([P, TOKEN_TILES, HALF], F32, tag="t4")
-            res = rope.tile([P, TOKEN_TILES, HEAD], F32, tag="rot", bufs=2)
-            nc.vector.tensor_tensor(out=t1[:], in0=y1, in1=cos_sb[:], op=ALU.mult)
-            nc.vector.tensor_tensor(out=t2[:], in0=y2, in1=sin_sb[:], op=ALU.mult)
-            nc.vector.tensor_tensor(out=t3[:], in0=y1, in1=sin_sb[:], op=ALU.mult)
-            nc.vector.tensor_tensor(out=t4[:], in0=y2, in1=cos_sb[:], op=ALU.mult)
-            nc.vector.tensor_tensor(out=res[:, :, 0:HALF], in0=t1[:], in1=t2[:], op=ALU.subtract)
-            nc.vector.tensor_tensor(out=res[:, :, HALF:HEAD], in0=t3[:], in1=t4[:], op=ALU.add)
-            nc.sync.dma_start(out=dst.rearrange("o (m p) c -> p (o m) c", p=P), in_=res[:])
+        def rotate():
+            ys = []
+            for a in range(2):
+                y = rope.tile([P, TOKEN_TILES, HEAD], F32, name="y%d" % a)
+                nc.vector.tensor_tensor(
+                    out=y[:],
+                    in0=qk_act[:],
+                    in1=gains[:, a, :].unsqueeze(1).to_broadcast([P, TOKEN_TILES, HEAD]),
+                    op=ALU.mult,
+                )
+                ys.append(y)
+            for a, dst in enumerate((out_2, out_3)):
+                pairs = ys[a][:].rearrange("p m (i e) -> p m i e", e=2)
+                y1 = pairs[:, :, :, 0]
+                y2 = pairs[:, :, :, 1]
+                t1 = rope.tile([P, TOKEN_TILES, HALF], F32, tag="t1")
+                t2 = rope.tile([P, TOKEN_TILES, HALF], F32, tag="t2")
+                t3 = rope.tile([P, TOKEN_TILES, HALF], F32, tag="t3")
+                t4 = rope.tile([P, TOKEN_TILES, HALF], F32, tag="t4")
+                res = rope.tile([P, TOKEN_TILES, HEAD], F32, tag="rot", bufs=2)
+                nc.vector.tensor_tensor(out=t1[:], in0=y1, in1=cos_sb[:], op=ALU.mult)
+                nc.vector.tensor_tensor(out=t2[:], in0=y2, in1=sin_sb[:], op=ALU.mult)
+                nc.vector.tensor_tensor(out=t3[:], in0=y1, in1=sin_sb[:], op=ALU.mult)
+                nc.vector.tensor_tensor(out=t4[:], in0=y2, in1=cos_sb[:], op=ALU.mult)
+                nc.vector.tensor_tensor(out=res[:, :, 0:HALF], in0=t1[:], in1=t2[:], op=ALU.subtract)
+                nc.vector.tensor_tensor(out=res[:, :, HALF:HEAD], in0=t3[:], in1=t4[:], op=ALU.add)
+                nc.sync.dma_start(out=dst.rearrange("o (p m) c -> p (o m) c", m=TOKEN_TILES), in_=res[:])
 
         for m in range(TOKEN_TILES):
             turn_x(m)
-        widen(0)
-        for i in range(len(units)):
-            interleave(i)
-            if i + 1 < len(units):
-                widen(i + 1)
-            quantise_w(i)
-            if i == 0:
-                for m in range(3):
-                    quantise_x(m)
-            if i == 1:
-                for m in range(3, TOKEN_TILES):
-                    quantise_x(m)
-            if i >= LAG and units[i - LAG][1] == PASSES - 1:
-                chunk(units[i - LAG][0])
-        chunk(len(CHUNKS) - 1)
-        rotate(0, out_2)
-        rotate(1, out_3)
+        widen(0, True)
+        for n, (c0, width) in enumerate(GROUPS):
+            widen(n, False)
+            if n + 1 < len(GROUPS):
+                widen(n + 1, True)
+            for off in range(0, width, N_TILE):
+                w = min(N_TILE, width - off)
+                codes, scales = quantise_w(n, off, w)
+                if n == 0:
+                    for h in range(TOKEN_TILES // 2):
+                        quantise_x(h)
+                chunk(c0 + off, w, codes, scales)
+        rotate()

@@ -24,8 +24,8 @@ HALF = HEAD // 2
 N_TILE = 512
 
 GROUPS = ((0, 512), (2560, 640), (512, 1024), (1536, 1024))
-SCALAR_PLANES = ((0, 0), (1, 1), (1, 2), (1, 2))
 RES_BUFS = 16
+TENSOR_PASSES = (1,)
 
 
 def tile_gatedattentionunit_pa_kernel(
@@ -55,6 +55,8 @@ def tile_gatedattentionunit_pa_kernel(
         nc.vector.memset(ones[:], 1.0)
         ident = const.tile([P, P], F32, name="ident")
         make_identity(nc, ident[:])
+        ident_bf = const.tile([P, P], BF16, name="ident_bf")
+        make_identity(nc, ident_bf[:])
 
         x_view = hidden_states.rearrange("o (p m) k -> p (o m) k", m=TOKEN_TILES)
         w_view = W_i_bytes.rearrange("(g p t) n -> g p t n", p=P, t=PACK)
@@ -79,7 +81,7 @@ def tile_gatedattentionunit_pa_kernel(
         nc.sync.dma_start(out=cos_sb[:], in_=cos.rearrange("o (p m) i -> p (o m) i", m=TOKEN_TILES))
         nc.sync.dma_start(out=sin_sb[:], in_=sin.rearrange("o (p m) i -> p (o m) i", m=TOKEN_TILES))
 
-        gain_ps = psum.tile([P, 2, HEAD], F32, tag="acc", bufs=6)
+        gain_ps = psum.tile([P, 2, HEAD], F32, tag="acc", bufs=5)
         nc.tensor.matmul(
             out=gain_ps[:].rearrange("p a c -> p (a c)"),
             lhsT=ones[:],
@@ -87,8 +89,8 @@ def tile_gatedattentionunit_pa_kernel(
             start=True,
             stop=True,
         )
-        gains = const.tile([P, 2, HEAD], F32, name="gains")
-        nc.scalar.copy(out=gains[:], in_=gain_ps[:])
+        gains = const.tile([P, 2, 2, HALF], F32, name="gains")
+        nc.scalar.copy(out=gains[:], in_=gain_ps[:].rearrange("p a (i e) -> p a e i", e=2))
 
         x_codes = [keep.tile([P, 2 * PASSES * P], U32, name="x_codes%d" % h, align_bytes=64) for h in range(TOKEN_TILES // 2)]
         x_scales = [keep.tile([P, 2 * PASSES * P], U8, name="x_scales%d" % h, align_bytes=64) for h in range(TOKEN_TILES // 2)]
@@ -97,7 +99,7 @@ def tile_gatedattentionunit_pa_kernel(
         def turn_x(m):
             h, a = divmod(m, 2)
             words = x_sb[h][:, a, :].bitcast(F32)
-            xt = psum.tile([P, PASSES, 2, P], F32, tag="xt", bufs=2)
+            xt = psum.tile([P, PASSES, 2, P], F32, tag="xt", bufs=3)
             for g in range(PASSES):
                 for u in range(2):
                     nc.tensor.transpose(
@@ -118,38 +120,50 @@ def tile_gatedattentionunit_pa_kernel(
 
         w_planes = {}
 
-        def widen(n, scalar_share):
+        def widen(n):
             c0, width = GROUPS[n]
-            for g in range(PASSES):
-                if (n, g) not in w_planes:
-                    w_planes[(n, g)] = stage.tile([P, PACK, width], BF16, tag="w_planes", bufs=4, align_bytes=64, name="w_planes")
-                planes = w_planes[(n, g)]
+            for g in reversed(range(PASSES)):
+                planes = stage.tile([P, PACK, width], BF16, tag="w_planes", bufs=4, align_bytes=64)
                 for t in range(PACK):
-                    codes = w_bytes[n][g][:, t, :].bitcast(FP8)
-                    on_scalar = t >= PACK - SCALAR_PLANES[n][g]
-                    if on_scalar and scalar_share:
-                        nc.scalar.activation(
-                            out=planes[:, t, :], in_=codes, func=ACT.Copy, scale=w_scale[:, g, t : t + 1]
-                        )
-                    if not on_scalar and not scalar_share:
-                        nc.vector.tensor_scalar(
-                            out=planes[:, t, :],
-                            in0=codes,
-                            scalar1=w_scale[:, g, t : t + 1],
-                            scalar2=None,
-                            op0=ALU.mult,
-                        )
+                    nc.vector.tensor_scalar(
+                        out=planes[:, t, :],
+                        in0=w_bytes[n][g][:, t, :].bitcast(FP8),
+                        scalar1=w_scale[:, g, t : t + 1],
+                        scalar2=None,
+                        op0=ALU.mult,
+                    )
+                w_planes[(n, g)] = planes
 
         def quantise_w(n, off, w):
             codes = keep.tile([P, PASSES * w], U32, name="w_codes%d_%d" % (n, off), align_bytes=64)
             scales = keep.tile([P, PASSES * w], U8, name="w_scales%d_%d" % (n, off), align_bytes=64)
-            grouped = []
-            for g in range(PASSES):
+            grouped = {}
+            for g in reversed(range(PASSES)):
                 gr = stage.tile([P, w, PACK], BF16, tag="w_grouped", bufs=4, align_bytes=64)
-                nc.vector.tensor_copy(
-                    out=gr[:], in_=w_planes[(n, g)][:, :, off : off + w].rearrange("p t c -> p c t")
-                )
-                grouped.append(gr)
+                planes = w_planes[(n, g)]
+                if w == HEAD:
+                    nc.vector.tensor_copy(
+                        out=gr[:].rearrange("p (e i) t -> p e i t", e=2),
+                        in_=planes[:, :, off : off + w].rearrange("p t (i e) -> p e i t", e=2),
+                    )
+                elif g in TENSOR_PASSES:
+                    for b in range(0, w, 256):
+                        turned = psum.tile([P, 256, PACK], BF16, tag="xt", bufs=3)
+                        for s in range(0, 256, P):
+                            c = off + b + s
+                            nc.tensor.matmul(
+                                out=turned[:, s : s + P, :],
+                                lhsT=ident_bf[:],
+                                rhs=planes[:, :, c : c + P].rearrange("p t c -> p c t"),
+                                start=True,
+                                stop=True,
+                            )
+                        nc.scalar.copy(out=gr[:, b : b + 256, :], in_=turned[:])
+                else:
+                    nc.vector.tensor_copy(
+                        out=gr[:], in_=planes[:, :, off : off + w].rearrange("p t c -> p c t")
+                    )
+                grouped[g] = gr
             for g in range(PASSES):
                 nc.vector.quantize_mx(
                     out=codes[:, g * w : (g + 1) * w].bitcast(FP8X4),
@@ -178,54 +192,54 @@ def tile_gatedattentionunit_pa_kernel(
         def chunk(c, w, codes, scales):
             if c >= 2 * EXPAND:
                 for h in range(TOKEN_TILES // 4):
-                    acc = psum.tile([P, 4, HEAD], F32, tag="acc", bufs=6)
+                    acc = psum.tile([P, 4, HEAD], F32, tag="acc", bufs=5)
                     for r in range(4):
                         product(acc[:, r, :], codes, scales, w, 4 * h + r)
                     nc.scalar.activation(out=qk_act[:, 4 * h : 4 * h + 4, :], in_=acc[:], func=ACT.Silu)
                 return
             o, d0 = divmod(c, EXPAND)
             for m in range(TOKEN_TILES):
-                acc = psum.tile([P, w], F32, tag="acc", bufs=6)
+                acc = psum.tile([P, w], F32, tag="acc", bufs=5)
                 product(acc[:], codes, scales, w, m)
                 res = outp.tile([P, w], F32, tag="res")
                 nc.scalar.activation(out=res[:], in_=acc[:], func=ACT.Silu)
                 nc.sync.dma_start(out=out_views[o][m][:, d0 : d0 + w], in_=res[:])
 
         def rotate():
-            ys = []
+            y = rope.tile([P, 2, TOKEN_TILES, HEAD], F32, name="y")
+            nc.vector.tensor_tensor(
+                out=y[:],
+                in0=qk_act[:].unsqueeze(1).to_broadcast([P, 2, TOKEN_TILES, HEAD]),
+                in1=gains[:].rearrange("p a e i -> p a (e i)").unsqueeze(2).to_broadcast([P, 2, TOKEN_TILES, HEAD]),
+                op=ALU.mult,
+            )
+            by_cos = []
+            by_sin = []
             for a in range(2):
-                y = rope.tile([P, TOKEN_TILES, HEAD], F32, name="y%d" % a)
-                nc.vector.tensor_tensor(
-                    out=y[:],
-                    in0=qk_act[:],
-                    in1=gains[:, a, :].unsqueeze(1).to_broadcast([P, TOKEN_TILES, HEAD]),
-                    op=ALU.mult,
-                )
-                ys.append(y)
+                halves = y[:, a].rearrange("p m (e i) -> p m e i", e=2)
+                for table, products, nm in ((cos_sb, by_cos, "c"), (sin_sb, by_sin, "s")):
+                    pr = rope.tile([P, TOKEN_TILES, 2, HALF], F32, name="y%s%d" % (nm, a))
+                    nc.vector.tensor_tensor(
+                        out=pr[:],
+                        in0=halves,
+                        in1=table[:].unsqueeze(2).to_broadcast([P, TOKEN_TILES, 2, HALF]),
+                        op=ALU.mult,
+                    )
+                    products.append(pr)
             for a, dst in enumerate((out_2, out_3)):
-                pairs = ys[a][:].rearrange("p m (i e) -> p m i e", e=2)
-                y1 = pairs[:, :, :, 0]
-                y2 = pairs[:, :, :, 1]
-                t1 = rope.tile([P, TOKEN_TILES, HALF], F32, tag="t1")
-                t2 = rope.tile([P, TOKEN_TILES, HALF], F32, tag="t2")
-                t3 = rope.tile([P, TOKEN_TILES, HALF], F32, tag="t3")
-                t4 = rope.tile([P, TOKEN_TILES, HALF], F32, tag="t4")
-                res = rope.tile([P, TOKEN_TILES, HEAD], F32, tag="rot", bufs=2)
-                nc.vector.tensor_tensor(out=t1[:], in0=y1, in1=cos_sb[:], op=ALU.mult)
-                nc.vector.tensor_tensor(out=t2[:], in0=y2, in1=sin_sb[:], op=ALU.mult)
-                nc.vector.tensor_tensor(out=t3[:], in0=y1, in1=sin_sb[:], op=ALU.mult)
-                nc.vector.tensor_tensor(out=t4[:], in0=y2, in1=cos_sb[:], op=ALU.mult)
-                nc.vector.tensor_tensor(out=res[:, :, 0:HALF], in0=t1[:], in1=t2[:], op=ALU.subtract)
-                nc.vector.tensor_tensor(out=res[:, :, HALF:HEAD], in0=t3[:], in1=t4[:], op=ALU.add)
+                res = rope.tile([P, TOKEN_TILES, HEAD], F32, name="rot%d" % a)
+                nc.vector.tensor_tensor(
+                    out=res[:, :, 0:HALF], in0=by_cos[a][:, :, 0, :], in1=by_sin[a][:, :, 1, :], op=ALU.subtract
+                )
+                nc.vector.tensor_tensor(
+                    out=res[:, :, HALF:HEAD], in0=by_sin[a][:, :, 0, :], in1=by_cos[a][:, :, 1, :], op=ALU.add
+                )
                 nc.sync.dma_start(out=dst.rearrange("o (p m) c -> p (o m) c", m=TOKEN_TILES), in_=res[:])
 
         for m in range(TOKEN_TILES):
             turn_x(m)
-        widen(0, True)
         for n, (c0, width) in enumerate(GROUPS):
-            widen(n, False)
-            if n + 1 < len(GROUPS):
-                widen(n + 1, True)
+            widen(n)
             for off in range(0, width, N_TILE):
                 w = min(N_TILE, width - off)
                 codes, scales = quantise_w(n, off, w)

@@ -24,8 +24,8 @@ HALF = HEAD // 2
 N_TILE = 512
 
 GROUPS = ((0, 512), (2560, 640), (512, 1024), (1536, 1024))
+SCALAR_PLANES = ((2, 2), (1, 1), (1, 2), (0, 1))
 RES_BUFS = 16
-TENSOR_PASSES = (1,)
 
 
 def tile_gatedattentionunit_pa_kernel(
@@ -55,8 +55,6 @@ def tile_gatedattentionunit_pa_kernel(
         nc.vector.memset(ones[:], 1.0)
         ident = const.tile([P, P], F32, name="ident")
         make_identity(nc, ident[:])
-        ident_bf = const.tile([P, P], BF16, name="ident_bf")
-        make_identity(nc, ident_bf[:])
 
         x_view = hidden_states.rearrange("o (p m) k -> p (o m) k", m=TOKEN_TILES)
         w_view = W_i_bytes.rearrange("(g p t) n -> g p t n", p=P, t=PACK)
@@ -81,7 +79,7 @@ def tile_gatedattentionunit_pa_kernel(
         nc.sync.dma_start(out=cos_sb[:], in_=cos.rearrange("o (p m) i -> p (o m) i", m=TOKEN_TILES))
         nc.sync.dma_start(out=sin_sb[:], in_=sin.rearrange("o (p m) i -> p (o m) i", m=TOKEN_TILES))
 
-        gain_ps = psum.tile([P, 2, HEAD], F32, tag="acc", bufs=5)
+        gain_ps = psum.tile([P, 2, HEAD], F32, tag="acc", bufs=6)
         nc.tensor.matmul(
             out=gain_ps[:].rearrange("p a c -> p (a c)"),
             lhsT=ones[:],
@@ -99,7 +97,7 @@ def tile_gatedattentionunit_pa_kernel(
         def turn_x(m):
             h, a = divmod(m, 2)
             words = x_sb[h][:, a, :].bitcast(F32)
-            xt = psum.tile([P, PASSES, 2, P], F32, tag="xt", bufs=3)
+            xt = psum.tile([P, PASSES, 2, P], F32, tag="xt", bufs=2)
             for g in range(PASSES):
                 for u in range(2):
                     nc.tensor.transpose(
@@ -120,25 +118,33 @@ def tile_gatedattentionunit_pa_kernel(
 
         w_planes = {}
 
-        def widen(n):
+        def widen(n, scalar_share):
             c0, width = GROUPS[n]
-            for g in reversed(range(PASSES)):
-                planes = stage.tile([P, PACK, width], BF16, tag="w_planes", bufs=4, align_bytes=64)
+            for g in range(PASSES):
+                if (n, g) not in w_planes:
+                    w_planes[(n, g)] = stage.tile([P, PACK, width], BF16, tag="w_planes", bufs=4, align_bytes=64, name="w_planes")
+                planes = w_planes[(n, g)]
                 for t in range(PACK):
-                    nc.vector.tensor_scalar(
-                        out=planes[:, t, :],
-                        in0=w_bytes[n][g][:, t, :].bitcast(FP8),
-                        scalar1=w_scale[:, g, t : t + 1],
-                        scalar2=None,
-                        op0=ALU.mult,
-                    )
-                w_planes[(n, g)] = planes
+                    codes = w_bytes[n][g][:, t, :].bitcast(FP8)
+                    on_scalar = t >= PACK - SCALAR_PLANES[n][g]
+                    if on_scalar and scalar_share:
+                        nc.scalar.activation(
+                            out=planes[:, t, :], in_=codes, func=ACT.Copy, scale=w_scale[:, g, t : t + 1]
+                        )
+                    if not on_scalar and not scalar_share:
+                        nc.vector.tensor_scalar(
+                            out=planes[:, t, :],
+                            in0=codes,
+                            scalar1=w_scale[:, g, t : t + 1],
+                            scalar2=None,
+                            op0=ALU.mult,
+                        )
 
         def quantise_w(n, off, w):
             codes = keep.tile([P, PASSES * w], U32, name="w_codes%d_%d" % (n, off), align_bytes=64)
             scales = keep.tile([P, PASSES * w], U8, name="w_scales%d_%d" % (n, off), align_bytes=64)
-            grouped = {}
-            for g in reversed(range(PASSES)):
+            grouped = []
+            for g in range(PASSES):
                 gr = stage.tile([P, w, PACK], BF16, tag="w_grouped", bufs=4, align_bytes=64)
                 planes = w_planes[(n, g)]
                 if w == HEAD:
@@ -146,24 +152,11 @@ def tile_gatedattentionunit_pa_kernel(
                         out=gr[:].rearrange("p (e i) t -> p e i t", e=2),
                         in_=planes[:, :, off : off + w].rearrange("p t (i e) -> p e i t", e=2),
                     )
-                elif g in TENSOR_PASSES:
-                    for b in range(0, w, 256):
-                        turned = psum.tile([P, 256, PACK], BF16, tag="xt", bufs=3)
-                        for s in range(0, 256, P):
-                            c = off + b + s
-                            nc.tensor.matmul(
-                                out=turned[:, s : s + P, :],
-                                lhsT=ident_bf[:],
-                                rhs=planes[:, :, c : c + P].rearrange("p t c -> p c t"),
-                                start=True,
-                                stop=True,
-                            )
-                        nc.scalar.copy(out=gr[:, b : b + 256, :], in_=turned[:])
                 else:
                     nc.vector.tensor_copy(
                         out=gr[:], in_=planes[:, :, off : off + w].rearrange("p t c -> p c t")
                     )
-                grouped[g] = gr
+                grouped.append(gr)
             for g in range(PASSES):
                 nc.vector.quantize_mx(
                     out=codes[:, g * w : (g + 1) * w].bitcast(FP8X4),
@@ -192,14 +185,14 @@ def tile_gatedattentionunit_pa_kernel(
         def chunk(c, w, codes, scales):
             if c >= 2 * EXPAND:
                 for h in range(TOKEN_TILES // 4):
-                    acc = psum.tile([P, 4, HEAD], F32, tag="acc", bufs=5)
+                    acc = psum.tile([P, 4, HEAD], F32, tag="acc", bufs=6)
                     for r in range(4):
                         product(acc[:, r, :], codes, scales, w, 4 * h + r)
                     nc.scalar.activation(out=qk_act[:, 4 * h : 4 * h + 4, :], in_=acc[:], func=ACT.Silu)
                 return
             o, d0 = divmod(c, EXPAND)
             for m in range(TOKEN_TILES):
-                acc = psum.tile([P, w], F32, tag="acc", bufs=5)
+                acc = psum.tile([P, w], F32, tag="acc", bufs=6)
                 product(acc[:], codes, scales, w, m)
                 res = outp.tile([P, w], F32, tag="res")
                 nc.scalar.activation(out=res[:], in_=acc[:], func=ACT.Silu)
@@ -238,8 +231,11 @@ def tile_gatedattentionunit_pa_kernel(
 
         for m in range(TOKEN_TILES):
             turn_x(m)
+        widen(0, True)
         for n, (c0, width) in enumerate(GROUPS):
-            widen(n)
+            widen(n, False)
+            if n + 1 < len(GROUPS):
+                widen(n + 1, True)
             for off in range(0, width, N_TILE):
                 w = min(N_TILE, width - off)
                 codes, scales = quantise_w(n, off, w)

@@ -24,7 +24,7 @@ HALF = HEAD // 2
 N_TILE = 512
 
 GROUPS = ((0, 512), (2560, 640), (512, 1024), (1536, 1024))
-SCALAR_PLANES = ((2, 2), (1, 1), (1, 2), (0, 1))
+SCALAR_PLANES = ((2, 2), (1, 1), (1, 2), (0, 0))
 RES_BUFS = 16
 
 
@@ -64,16 +64,20 @@ def tile_gatedattentionunit_pa_kernel(
             for n, (c0, width) in enumerate(GROUPS)
         ]
 
-        def load_w(n):
+        def load_w(n, parts):
             c0, width = GROUPS[n]
+            step = PACK // parts
             for g in range(PASSES):
-                nc.sync.dma_start(out=w_bytes[n][g][:], in_=w_view[g][:, :, c0 : c0 + width])
+                for t in range(0, PACK, step):
+                    nc.sync.dma_start(
+                        out=w_bytes[n][g][:, t : t + step, :], in_=w_view[g][:, t : t + step, c0 : c0 + width]
+                    )
 
-        load_w(0)
+        load_w(0, 2)
         for h in range(TOKEN_TILES // 2):
             nc.sync.dma_start(out=x_sb[h][:], in_=x_view[:, 2 * h : 2 * h + 2, :])
         for n in range(1, len(GROUPS)):
-            load_w(n)
+            load_w(n, 1)
         cos_sb = const.tile([P, TOKEN_TILES, HALF], BF16, name="cos_sb")
         sin_sb = const.tile([P, TOKEN_TILES, HALF], BF16, name="sin_sb")
         nc.sync.dma_start(out=cos_sb[:], in_=cos.rearrange("o (p m) i -> p (o m) i", m=TOKEN_TILES))
@@ -154,7 +158,8 @@ def tile_gatedattentionunit_pa_kernel(
                     )
                 else:
                     nc.vector.tensor_copy(
-                        out=gr[:], in_=planes[:, :, off : off + w].rearrange("p t c -> p c t")
+                        out=gr[:].rearrange("p (c i) t -> p c t i", i=4),
+                        in_=planes[:, :, off : off + w].rearrange("p t (c i) -> p c t i", i=4),
                     )
                 grouped.append(gr)
             for g in range(PASSES):
@@ -221,13 +226,15 @@ def tile_gatedattentionunit_pa_kernel(
                     products.append(pr)
             for a, dst in enumerate((out_2, out_3)):
                 res = rope.tile([P, TOKEN_TILES, HEAD], F32, name="rot%d" % a)
-                nc.vector.tensor_tensor(
-                    out=res[:, :, 0:HALF], in0=by_cos[a][:, :, 0, :], in1=by_sin[a][:, :, 1, :], op=ALU.subtract
-                )
-                nc.vector.tensor_tensor(
-                    out=res[:, :, HALF:HEAD], in0=by_sin[a][:, :, 0, :], in1=by_cos[a][:, :, 1, :], op=ALU.add
-                )
-                nc.sync.dma_start(out=dst.rearrange("o (p m) c -> p (o m) c", m=TOKEN_TILES), in_=res[:])
+                view = dst.rearrange("o (p m) c -> p (o m) c", m=TOKEN_TILES)
+                for ms in ((slice(0, TOKEN_TILES),) if a == 0 else (slice(0, 4), slice(4, TOKEN_TILES))):
+                    nc.vector.tensor_tensor(
+                        out=res[:, ms, 0:HALF], in0=by_cos[a][:, ms, 0, :], in1=by_sin[a][:, ms, 1, :], op=ALU.subtract
+                    )
+                    nc.vector.tensor_tensor(
+                        out=res[:, ms, HALF:HEAD], in0=by_sin[a][:, ms, 0, :], in1=by_cos[a][:, ms, 1, :], op=ALU.add
+                    )
+                    nc.sync.dma_start(out=view[:, ms, :], in_=res[:, ms, :])
 
         for m in range(TOKEN_TILES):
             turn_x(m)

@@ -26,6 +26,7 @@ N_TILE = 512
 GROUPS = ((0, 512), (2560, 640), (512, 1024), (1536, 1024))
 SCALAR_PLANES = ((2, 2), (1, 1), (1, 2), (0, 0))
 RES_BUFS = 16
+LATE_BYTES = 4096
 
 
 def tile_gatedattentionunit_pa_kernel(
@@ -38,6 +39,7 @@ def tile_gatedattentionunit_pa_kernel(
         stage = ctx.enter_context(tc.tile_pool(name="stage", bufs=4))
         outp = ctx.enter_context(tc.tile_pool(name="outp", bufs=RES_BUFS))
         rope = ctx.enter_context(tc.tile_pool(name="rope", bufs=1))
+        late = ctx.enter_context(tc.tile_pool(name="late", bufs=1))
         psum = ctx.enter_context(tc.psum_pool(name="psum", bufs=2))
 
         w_scale = const.tile([P, PASSES, PACK], F32, name="w_scale")
@@ -55,6 +57,8 @@ def tile_gatedattentionunit_pa_kernel(
         nc.vector.memset(ones[:], 1.0)
         ident = const.tile([P, P], F32, name="ident")
         make_identity(nc, ident[:])
+        ident_bf = const.tile([P, P], BF16, name="ident_bf")
+        make_identity(nc, ident_bf[:])
 
         x_view = hidden_states.rearrange("o (p m) k -> p (o m) k", m=TOKEN_TILES)
         w_view = W_i_bytes.rearrange("(g p t) n -> g p t n", p=P, t=PACK)
@@ -82,17 +86,6 @@ def tile_gatedattentionunit_pa_kernel(
         sin_sb = const.tile([P, TOKEN_TILES, HALF], BF16, name="sin_sb")
         nc.sync.dma_start(out=cos_sb[:], in_=cos.rearrange("o (p m) i -> p (o m) i", m=TOKEN_TILES))
         nc.sync.dma_start(out=sin_sb[:], in_=sin.rearrange("o (p m) i -> p (o m) i", m=TOKEN_TILES))
-
-        gain_ps = psum.tile([P, 2, HEAD], F32, tag="acc", bufs=6)
-        nc.tensor.matmul(
-            out=gain_ps[:].rearrange("p a c -> p (a c)"),
-            lhsT=ones[:],
-            rhs=gain_row[:].rearrange("p a c -> p (a c)"),
-            start=True,
-            stop=True,
-        )
-        gains = const.tile([P, 2, 2, HALF], F32, name="gains")
-        nc.scalar.copy(out=gains[:], in_=gain_ps[:].rearrange("p a (i e) -> p a e i", e=2))
 
         x_codes = [keep.tile([P, 2 * PASSES * P], U32, name="x_codes%d" % h, align_bytes=64) for h in range(TOKEN_TILES // 2)]
         x_scales = [keep.tile([P, 2 * PASSES * P], U8, name="x_scales%d" % h, align_bytes=64) for h in range(TOKEN_TILES // 2)]
@@ -144,12 +137,15 @@ def tile_gatedattentionunit_pa_kernel(
                             op0=ALU.mult,
                         )
 
-        def quantise_w(n, off, w):
+        def quantise_w(n, off, w, last):
             codes = keep.tile([P, PASSES * w], U32, name="w_codes%d_%d" % (n, off), align_bytes=64)
             scales = keep.tile([P, PASSES * w], U8, name="w_scales%d_%d" % (n, off), align_bytes=64)
             grouped = []
             for g in range(PASSES):
-                gr = stage.tile([P, w, PACK], BF16, tag="w_grouped", bufs=4, align_bytes=64)
+                if last:
+                    gr = late.tile([P, w, PACK], BF16, name="last_grouped%d" % g, offset=g * LATE_BYTES, align_bytes=64)
+                else:
+                    gr = stage.tile([P, w, PACK], BF16, tag="w_grouped", bufs=4, align_bytes=64, name="w_grouped")
                 planes = w_planes[(n, g)]
                 if w == HEAD:
                     nc.vector.tensor_copy(
@@ -203,38 +199,79 @@ def tile_gatedattentionunit_pa_kernel(
                 nc.scalar.activation(out=res[:], in_=acc[:], func=ACT.Silu)
                 nc.sync.dma_start(out=out_views[o][m][:, d0 : d0 + w], in_=res[:])
 
+        tables = {}
+
+        def tables_to_psum():
+            trig = psum.tile([P, 2, TOKEN_TILES, HALF], BF16, tag="xt", bufs=2, name="trig")
+            for s, table in enumerate((cos_sb, sin_sb)):
+                nc.tensor.matmul(
+                    out=trig[:, s].rearrange("p m i -> p (m i)"),
+                    lhsT=ident_bf[:],
+                    rhs=table[:].rearrange("p m i -> p (m i)"),
+                    start=True,
+                    stop=True,
+                )
+            gains = psum.tile([P, 2, HEAD], F32, tag="xt", bufs=2, name="gains")
+            for a in range(2):
+                nc.tensor.matmul(
+                    out=gains[:, a, :],
+                    lhsT=ones[:],
+                    rhs=gain_row[:, a, :].rearrange("p (i e) -> p e i", e=2),
+                    start=True,
+                    stop=True,
+                )
+            gains_sb = const.tile([P, 2, HEAD], F32, name="gains_sb")
+            nc.scalar.copy(out=gains_sb[:], in_=gains[:])
+            tables["trig"] = trig
+            tables["gains"] = gains
+            tables["gains_sb"] = gains_sb
+
         def rotate():
-            y = rope.tile([P, 2, TOKEN_TILES, HEAD], F32, name="y")
+            trig, gains, gains_sb = tables["trig"], tables["gains"], tables["gains_sb"]
+            views = [o.rearrange("o (p m) c -> p (o m) c", m=TOKEN_TILES) for o in (out_2, out_3)]
+            hm = TOKEN_TILES // 2
+            y = [late.tile([P, hm, 2, HEAD], F32, name="y%d" % f, offset=f * LATE_BYTES, align_bytes=64) for f in range(2)]
             nc.vector.tensor_tensor(
-                out=y[:],
-                in0=qk_act[:].unsqueeze(1).to_broadcast([P, 2, TOKEN_TILES, HEAD]),
-                in1=gains[:].rearrange("p a e i -> p a (e i)").unsqueeze(2).to_broadcast([P, 2, TOKEN_TILES, HEAD]),
+                out=y[0][:],
+                in0=qk_act[:, 0:hm, :].unsqueeze(2).to_broadcast([P, hm, 2, HEAD]),
+                in1=gains[:].unsqueeze(1).to_broadcast([P, hm, 2, HEAD]),
                 op=ALU.mult,
             )
-            by_cos = []
-            by_sin = []
-            for a in range(2):
-                halves = y[:, a].rearrange("p m (e i) -> p m e i", e=2)
-                for table, products, nm in ((cos_sb, by_cos, "c"), (sin_sb, by_sin, "s")):
-                    pr = rope.tile([P, TOKEN_TILES, 2, HALF], F32, name="y%s%d" % (nm, a))
+            nc.gpsimd.tensor_tensor(
+                out=y[1][:],
+                in0=qk_act[:, hm:TOKEN_TILES, :].unsqueeze(2).to_broadcast([P, hm, 2, HEAD]),
+                in1=gains_sb[:].unsqueeze(1).to_broadcast([P, hm, 2, HEAD]),
+                op=ALU.mult,
+            )
+            by = []
+            for f in range(2):
+                for s in range(2):
+                    pr = rope.tile([P, hm, 2, 2, HALF], F32, name="by%d_%d" % (f, s))
                     nc.vector.tensor_tensor(
-                        out=pr[:],
-                        in0=halves,
-                        in1=table[:].unsqueeze(2).to_broadcast([P, TOKEN_TILES, 2, HALF]),
+                        out=pr[:].rearrange("p m a e i -> p m (a e) i"),
+                        in0=y[f][:].rearrange("p m a (e i) -> p m (a e) i", e=2),
+                        in1=trig[:, s, f * hm : (f + 1) * hm, :].unsqueeze(2).to_broadcast([P, hm, 4, HALF]),
                         op=ALU.mult,
                     )
-                    products.append(pr)
-            for a, dst in enumerate((out_2, out_3)):
-                res = rope.tile([P, TOKEN_TILES, HEAD], F32, name="rot%d" % a)
-                view = dst.rearrange("o (p m) c -> p (o m) c", m=TOKEN_TILES)
-                for ms in ((slice(0, TOKEN_TILES),) if a == 0 else (slice(0, 4), slice(4, TOKEN_TILES))):
-                    nc.vector.tensor_tensor(
-                        out=res[:, ms, 0:HALF], in0=by_cos[a][:, ms, 0, :], in1=by_sin[a][:, ms, 1, :], op=ALU.subtract
+                    by.append(pr)
+            for f, eng in ((0, nc.gpsimd), (1, nc.vector)):
+                by_cos, by_sin = by[2 * f], by[2 * f + 1]
+                res = rope.tile([P, 2, hm, HEAD], F32, name="rot%d" % f)
+                for aa in ((slice(0, 2),) if f == 0 else (slice(0, 1), slice(1, 2))):
+                    eng.tensor_tensor(
+                        out=res[:, aa, :, 0:HALF],
+                        in0=by_cos[:, :, aa, 0, :].rearrange("p m a i -> p a m i"),
+                        in1=by_sin[:, :, aa, 1, :].rearrange("p m a i -> p a m i"),
+                        op=ALU.subtract,
                     )
-                    nc.vector.tensor_tensor(
-                        out=res[:, ms, HALF:HEAD], in0=by_sin[a][:, ms, 0, :], in1=by_cos[a][:, ms, 1, :], op=ALU.add
+                    eng.tensor_tensor(
+                        out=res[:, aa, :, HALF:HEAD],
+                        in0=by_sin[:, :, aa, 0, :].rearrange("p m a i -> p a m i"),
+                        in1=by_cos[:, :, aa, 1, :].rearrange("p m a i -> p a m i"),
+                        op=ALU.add,
                     )
-                    nc.sync.dma_start(out=view[:, ms, :], in_=res[:, ms, :])
+                    for a in range(aa.start, aa.stop):
+                        nc.sync.dma_start(out=views[a][:, f * hm : (f + 1) * hm, :], in_=res[:, a])
 
         for m in range(TOKEN_TILES):
             turn_x(m)
@@ -245,9 +282,11 @@ def tile_gatedattentionunit_pa_kernel(
                 widen(n + 1, True)
             for off in range(0, width, N_TILE):
                 w = min(N_TILE, width - off)
-                codes, scales = quantise_w(n, off, w)
+                codes, scales = quantise_w(n, off, w, n == len(GROUPS) - 1 and off + w == width)
                 if n == 0:
                     for h in range(TOKEN_TILES // 2):
                         quantise_x(h)
                 chunk(c0 + off, w, codes, scales)
+                if n == 2 and off == 0:
+                    tables_to_psum()
         rotate()

@@ -25,6 +25,7 @@ N_TILE = 512
 
 GROUPS = ((0, 512), (2560, 640), (512, 1024), (1536, 1024))
 SCALAR_PLANES = ((2, 2), (1, 1), (1, 2), (0, 0))
+UNITS = (((0, 512),), ((0, 512), (512, 128)), ((0, 512), (512, 512)), ((0, 512), (512, 256), (768, 256)))
 RES_BUFS = 16
 LATE_BYTES = 4096
 
@@ -183,6 +184,8 @@ def tile_gatedattentionunit_pa_kernel(
                     stop=(g == PASSES - 1),
                 )
 
+        results = {}
+
         def chunk(c, w, codes, scales):
             if c >= 2 * EXPAND:
                 for h in range(TOKEN_TILES // 4):
@@ -192,12 +195,16 @@ def tile_gatedattentionunit_pa_kernel(
                     nc.scalar.activation(out=qk_act[:, 4 * h : 4 * h + 4, :], in_=acc[:], func=ACT.Silu)
                 return
             o, d0 = divmod(c, EXPAND)
+            r0 = d0 % N_TILE
             for m in range(TOKEN_TILES):
                 acc = psum.tile([P, w], F32, tag="acc", bufs=6)
                 product(acc[:], codes, scales, w, m)
-                res = outp.tile([P, w], F32, tag="res")
-                nc.scalar.activation(out=res[:], in_=acc[:], func=ACT.Silu)
-                nc.sync.dma_start(out=out_views[o][m][:, d0 : d0 + w], in_=res[:])
+                if r0 == 0:
+                    results[m] = outp.tile([P, N_TILE], F32, tag="res", name="res")
+                res = results[m]
+                nc.scalar.activation(out=res[:, r0 : r0 + w], in_=acc[:], func=ACT.Silu)
+                if r0 + w == N_TILE:
+                    nc.sync.dma_start(out=out_views[o][m][:, d0 - r0 : d0 + w], in_=res[:])
 
         tables = {}
 
@@ -280,8 +287,7 @@ def tile_gatedattentionunit_pa_kernel(
             widen(n, False)
             if n + 1 < len(GROUPS):
                 widen(n + 1, True)
-            for off in range(0, width, N_TILE):
-                w = min(N_TILE, width - off)
+            for off, w in UNITS[n]:
                 codes, scales = quantise_w(n, off, w, n == len(GROUPS) - 1 and off + w == width)
                 if n == 0:
                     for h in range(TOKEN_TILES // 2):

@@ -23,9 +23,10 @@ TOKEN_TILES = TOKENS // P
 HALF = HEAD // 2
 N_TILE = 512
 
-GROUPS = ((0, 512), (2560, 640), (512, 1024), (1536, 1024))
-SCALAR_PLANES = ((2, 2), (1, 1), (1, 2), (0, 0))
-UNITS = (((0, 512),), ((0, 512), (512, 128)), ((0, 512), (512, 512)), ((0, 512), (512, 256), (768, 256)))
+LOADS = ((0, 512), (2560, 640), (512, 1024), (1536, 1024))
+GROUPS = ((0, 512, 0), (2560, 640, 1), (512, 1024, 2), (1536, 512, 3), (2048, 512, 3))
+SCALAR_PLANES = ((2, 2), (1, 0), (1, 1), (0, 0), (0, 0))
+UNITS = (((0, 512),), ((0, 512), (512, 128)), ((0, 512), (512, 512)), ((0, 512),), ((0, 256), (256, 256)))
 RES_BUFS = 16
 LATE_BYTES = 4096
 
@@ -66,11 +67,11 @@ def tile_gatedattentionunit_pa_kernel(
         x_sb = [keep.tile([P, 2, HIDDEN], BF16, name="x_sb%d" % h) for h in range(TOKEN_TILES // 2)]
         w_bytes = [
             [keep.tile([P, PACK, width], U8, name="w_bytes%d_%d" % (n, g)) for g in range(PASSES)]
-            for n, (c0, width) in enumerate(GROUPS)
+            for n, (c0, width) in enumerate(LOADS)
         ]
 
         def load_w(n, parts):
-            c0, width = GROUPS[n]
+            c0, width = LOADS[n]
             step = PACK // parts
             for g in range(PASSES):
                 for t in range(0, PACK, step):
@@ -81,7 +82,7 @@ def tile_gatedattentionunit_pa_kernel(
         load_w(0, 2)
         for h in range(TOKEN_TILES // 2):
             nc.sync.dma_start(out=x_sb[h][:], in_=x_view[:, 2 * h : 2 * h + 2, :])
-        for n in range(1, len(GROUPS)):
+        for n in range(1, len(LOADS)):
             load_w(n, 1)
         cos_sb = const.tile([P, TOKEN_TILES, HALF], BF16, name="cos_sb")
         sin_sb = const.tile([P, TOKEN_TILES, HALF], BF16, name="sin_sb")
@@ -117,13 +118,14 @@ def tile_gatedattentionunit_pa_kernel(
         w_planes = {}
 
         def widen(n, scalar_share):
-            c0, width = GROUPS[n]
+            c0, width, ld = GROUPS[n]
+            b0 = c0 - LOADS[ld][0]
             for g in range(PASSES):
                 if (n, g) not in w_planes:
                     w_planes[(n, g)] = stage.tile([P, PACK, width], BF16, tag="w_planes", bufs=4, align_bytes=64, name="w_planes")
                 planes = w_planes[(n, g)]
                 for t in range(PACK):
-                    codes = w_bytes[n][g][:, t, :].bitcast(FP8)
+                    codes = w_bytes[ld][g][:, t, b0 : b0 + width].bitcast(FP8)
                     on_scalar = t >= PACK - SCALAR_PLANES[n][g]
                     if on_scalar and scalar_share:
                         nc.scalar.activation(
@@ -184,8 +186,6 @@ def tile_gatedattentionunit_pa_kernel(
                     stop=(g == PASSES - 1),
                 )
 
-        results = {}
-
         def chunk(c, w, codes, scales):
             if c >= 2 * EXPAND:
                 for h in range(TOKEN_TILES // 4):
@@ -195,16 +195,12 @@ def tile_gatedattentionunit_pa_kernel(
                     nc.scalar.activation(out=qk_act[:, 4 * h : 4 * h + 4, :], in_=acc[:], func=ACT.Silu)
                 return
             o, d0 = divmod(c, EXPAND)
-            r0 = d0 % N_TILE
             for m in range(TOKEN_TILES):
                 acc = psum.tile([P, w], F32, tag="acc", bufs=6)
                 product(acc[:], codes, scales, w, m)
-                if r0 == 0:
-                    results[m] = outp.tile([P, N_TILE], F32, tag="res", name="res")
-                res = results[m]
-                nc.scalar.activation(out=res[:, r0 : r0 + w], in_=acc[:], func=ACT.Silu)
-                if r0 + w == N_TILE:
-                    nc.sync.dma_start(out=out_views[o][m][:, d0 - r0 : d0 + w], in_=res[:])
+                res = outp.tile([P, w], F32, tag="res")
+                nc.scalar.activation(out=res[:], in_=acc[:], func=ACT.Silu)
+                nc.sync.dma_start(out=out_views[o][m][:, d0 : d0 + w], in_=res[:])
 
         tables = {}
 
@@ -283,7 +279,7 @@ def tile_gatedattentionunit_pa_kernel(
         for m in range(TOKEN_TILES):
             turn_x(m)
         widen(0, True)
-        for n, (c0, width) in enumerate(GROUPS):
+        for n, (c0, width, ld) in enumerate(GROUPS):
             widen(n, False)
             if n + 1 < len(GROUPS):
                 widen(n + 1, True)

@@ -28,6 +28,8 @@ GROUPS = ((0, 512, 0), (2560, 640, 1), (512, 1024, 2), (1536, 512, 3), (2048, 51
 SCALAR_PLANES = ((2, 2), (1, 0), (1, 1), (0, 0), (0, 0))
 UNITS = (((0, 512),), ((0, 512), (512, 128)), ((0, 512), (512, 512)), ((0, 512),), ((0, 256), (256, 256)))
 RES_BUFS = 16
+WARM_BEFORE = 10
+WARM_BETWEEN = 2
 LATE_BYTES = 4096
 
 
@@ -59,6 +61,8 @@ def tile_gatedattentionunit_pa_kernel(
         nc.vector.memset(ones[:], 1.0)
         ident = const.tile([P, P], F32, name="ident")
         make_identity(nc, ident[:])
+        idle_rhs = const.tile([P, N_TILE], BF16, name="idle_rhs")
+        nc.vector.memset(idle_rhs[:], 0.0)
         ident_bf = const.tile([P, P], BF16, name="ident_bf")
         make_identity(nc, ident_bf[:])
 
@@ -107,6 +111,12 @@ def tile_gatedattentionunit_pa_kernel(
             nc.scalar.copy(
                 out=x_grouped[h][:, a].bitcast(F32), in_=xt[:].rearrange("p g u r -> p g r u")
             )
+
+        idle_ps = psum.tile([P, N_TILE], F32, tag="acc", bufs=6, name="idle_ps")
+
+        def keep_warm(count):
+            for i in range(count):
+                nc.tensor.matmul(out=idle_ps[:], lhsT=ones[:], rhs=idle_rhs[:], start=True, stop=True)
 
         def quantise_x(h):
             nc.vector.quantize_mx(
@@ -276,8 +286,11 @@ def tile_gatedattentionunit_pa_kernel(
                     for a in range(aa.start, aa.stop):
                         nc.sync.dma_start(out=views[a][:, f * hm : (f + 1) * hm, :], in_=res[:, a])
 
+        keep_warm(WARM_BEFORE)
         for m in range(TOKEN_TILES):
             turn_x(m)
+            if m % 2 == 1:
+                keep_warm(WARM_BETWEEN)
         widen(0, True)
         for n, (c0, width, ld) in enumerate(GROUPS):
             widen(n, False)

@@ -83,10 +83,16 @@ def tile_gatedattentionunit_pa_kernel(
                         out=w_bytes[n][g][:, t : t + step, :], in_=w_view[g][:, t : t + step, c0 : c0 + width]
                     )
 
-        load_w(0, 2)
-        for h in range(TOKEN_TILES // 2):
+        def load_x(h):
             nc.sync.dma_start(out=x_sb[h][:], in_=x_view[:, 2 * h : 2 * h + 2, :])
-        for n in range(1, len(LOADS)):
+
+        load_w(0, 2)
+        load_x(0)
+        load_x(1)
+        load_w(1, 1)
+        load_x(2)
+        load_x(3)
+        for n in range(2, len(LOADS)):
             load_w(n, 1)
         cos_sb = const.tile([P, TOKEN_TILES, HALF], BF16, name="cos_sb")
         sin_sb = const.tile([P, TOKEN_TILES, HALF], BF16, name="sin_sb")

@@ -24,9 +24,9 @@ HALF = HEAD // 2
 N_TILE = 512
 
 LOADS = ((0, 512), (2560, 640), (512, 1024), (1536, 1024))
-GROUPS = ((0, 512, 0), (2560, 640, 1), (512, 1024, 2), (1536, 512, 3), (2048, 512, 3))
-SCALAR_PLANES = ((2, 2), (1, 0), (1, 1), (0, 0), (0, 0))
-UNITS = (((0, 512),), ((0, 512), (512, 128)), ((0, 512), (512, 512)), ((0, 512),), ((0, 256), (256, 256)))
+GROUPS = ((0, 512, 0), (2560, 640, 1), (512, 1024, 2), (1536, 1024, 3))
+SCALAR_PLANES = ((2, 2), (1, 0), (1, 1), (0, 0))
+UNITS = (((0, 512),), ((0, 512), (512, 128)), ((0, 512), (512, 512)), ((0, 512), (512, 256), (768, 256)))
 RES_BUFS = 16
 WARM_BEFORE = 10
 WARM_BETWEEN = 2

@@ -28,6 +28,7 @@ GROUPS = ((0, 512, 0), (2560, 640, 1), (512, 1024, 2), (1536, 1024, 3))
 SCALAR_PLANES = ((2, 2), (1, 0), (1, 1), (0, 0))
 UNITS = (((0, 512),), ((0, 512), (512, 128)), ((0, 512), (512, 512)), ((0, 512), (512, 256), (768, 256)))
 RES_BUFS = 16
+BANKS = 8
 WARM_BEFORE = 10
 WARM_BETWEEN = 2
 LATE_BYTES = 4096
@@ -63,8 +64,6 @@ def tile_gatedattentionunit_pa_kernel(
         make_identity(nc, ident[:])
         idle_rhs = const.tile([P, N_TILE], BF16, name="idle_rhs")
         nc.vector.memset(idle_rhs[:], 0.0)
-        ident_bf = const.tile([P, P], BF16, name="ident_bf")
-        make_identity(nc, ident_bf[:])
 
         x_view = hidden_states.rearrange("o (p m) k -> p (o m) k", m=TOKEN_TILES)
         w_view = W_i_bytes.rearrange("(g p t) n -> g p t n", p=P, t=PACK)
@@ -106,7 +105,7 @@ def tile_gatedattentionunit_pa_kernel(
         def turn_x(m):
             h, a = divmod(m, 2)
             words = x_sb[h][:, a, :].bitcast(F32)
-            xt = psum.tile([P, PASSES, 2, P], F32, tag="xt", bufs=2)
+            xt = psum.tile([P, PASSES, 2, P], F32, tag="acc", bufs=BANKS)
             for g in range(PASSES):
                 for u in range(2):
                     nc.tensor.transpose(
@@ -118,7 +117,7 @@ def tile_gatedattentionunit_pa_kernel(
                 out=x_grouped[h][:, a].bitcast(F32), in_=xt[:].rearrange("p g u r -> p g r u")
             )
 
-        idle_ps = psum.tile([P, N_TILE], F32, tag="acc", bufs=6, name="idle_ps")
+        idle_ps = psum.tile([P, N_TILE], F32, tag="acc", bufs=BANKS, name="idle_ps")
 
         def keep_warm(count):
             for i in range(count):
@@ -205,14 +204,14 @@ def tile_gatedattentionunit_pa_kernel(
         def chunk(c, w, codes, scales):
             if c >= 2 * EXPAND:
                 for h in range(TOKEN_TILES // 4):
-                    acc = psum.tile([P, 4, HEAD], F32, tag="acc", bufs=6)
+                    acc = psum.tile([P, 4, HEAD], F32, tag="acc", bufs=BANKS)
                     for r in range(4):
                         product(acc[:, r, :], codes, scales, w, 4 * h + r)
                     nc.scalar.activation(out=qk_act[:, 4 * h : 4 * h + 4, :], in_=acc[:], func=ACT.Silu)
                 return
             o, d0 = divmod(c, EXPAND)
             for m in range(TOKEN_TILES):
-                acc = psum.tile([P, w], F32, tag="acc", bufs=6)
+                acc = psum.tile([P, w], F32, tag="acc", bufs=BANKS)
                 product(acc[:], codes, scales, w, m)
                 res = outp.tile([P, w], F32, tag="res")
                 nc.scalar.activation(out=res[:], in_=acc[:], func=ACT.Silu)
@@ -221,16 +220,7 @@ def tile_gatedattentionunit_pa_kernel(
         tables = {}
 
         def tables_to_psum():
-            trig = psum.tile([P, 2, TOKEN_TILES, HALF], BF16, tag="xt", bufs=2, name="trig")
-            for s, table in enumerate((cos_sb, sin_sb)):
-                nc.tensor.matmul(
-                    out=trig[:, s].rearrange("p m i -> p (m i)"),
-                    lhsT=ident_bf[:],
-                    rhs=table[:].rearrange("p m i -> p (m i)"),
-                    start=True,
-                    stop=True,
-                )
-            gains = psum.tile([P, 2, HEAD], F32, tag="xt", bufs=2, name="gains")
+            gains = psum.tile([P, 2, HEAD], F32, tag="acc", bufs=BANKS, name="gains")
             for a in range(2):
                 nc.tensor.matmul(
                     out=gains[:, a, :],
@@ -239,58 +229,41 @@ def tile_gatedattentionunit_pa_kernel(
                     start=True,
                     stop=True,
                 )
-            gains_sb = const.tile([P, 2, HEAD], F32, name="gains_sb")
-            nc.scalar.copy(out=gains_sb[:], in_=gains[:])
-            tables["trig"] = trig
             tables["gains"] = gains
-            tables["gains_sb"] = gains_sb
 
         def rotate():
-            trig, gains, gains_sb = tables["trig"], tables["gains"], tables["gains_sb"]
+            gains = tables["gains"]
             views = [o.rearrange("o (p m) c -> p (o m) c", m=TOKEN_TILES) for o in (out_2, out_3)]
             hm = TOKEN_TILES // 2
             y = [late.tile([P, hm, 2, HEAD], F32, name="y%d" % f, offset=f * LATE_BYTES, align_bytes=64) for f in range(2)]
-            nc.vector.tensor_tensor(
-                out=y[0][:],
-                in0=qk_act[:, 0:hm, :].unsqueeze(2).to_broadcast([P, hm, 2, HEAD]),
-                in1=gains[:].unsqueeze(1).to_broadcast([P, hm, 2, HEAD]),
-                op=ALU.mult,
-            )
-            nc.gpsimd.tensor_tensor(
-                out=y[1][:],
-                in0=qk_act[:, hm:TOKEN_TILES, :].unsqueeze(2).to_broadcast([P, hm, 2, HEAD]),
-                in1=gains_sb[:].unsqueeze(1).to_broadcast([P, hm, 2, HEAD]),
-                op=ALU.mult,
-            )
-            by = []
             for f in range(2):
-                for s in range(2):
+                nc.vector.tensor_tensor(
+                    out=y[f][:],
+                    in0=qk_act[:, f * hm : (f + 1) * hm, :].unsqueeze(2).to_broadcast([P, hm, 2, HEAD]),
+                    in1=gains[:].unsqueeze(1).to_broadcast([P, hm, 2, HEAD]),
+                    op=ALU.mult,
+                )
+            for f in range(2):
+                by = []
+                for s, table in enumerate((cos_sb, sin_sb)):
                     pr = rope.tile([P, hm, 2, 2, HALF], F32, name="by%d_%d" % (f, s))
                     nc.vector.tensor_tensor(
                         out=pr[:].rearrange("p m a e i -> p m (a e) i"),
                         in0=y[f][:].rearrange("p m a (e i) -> p m (a e) i", e=2),
-                        in1=trig[:, s, f * hm : (f + 1) * hm, :].unsqueeze(2).to_broadcast([P, hm, 4, HALF]),
+                        in1=table[:, f * hm : (f + 1) * hm, :].unsqueeze(2).to_broadcast([P, hm, 4, HALF]),
                         op=ALU.mult,
                     )
                     by.append(pr)
-            for f, eng in ((0, nc.gpsimd), (1, nc.vector)):
-                by_cos, by_sin = by[2 * f], by[2 * f + 1]
+                by_cos, by_sin = by
                 res = rope.tile([P, 2, hm, HEAD], F32, name="rot%d" % f)
-                for aa in ((slice(0, 2),) if f == 0 else (slice(0, 1), slice(1, 2))):
-                    eng.tensor_tensor(
-                        out=res[:, aa, :, 0:HALF],
-                        in0=by_cos[:, :, aa, 0, :].rearrange("p m a i -> p a m i"),
-                        in1=by_sin[:, :, aa, 1, :].rearrange("p m a i -> p a m i"),
-                        op=ALU.subtract,
+                for a in range(2):
+                    nc.vector.tensor_tensor(
+                        out=res[:, a, :, 0:HALF], in0=by_cos[:, :, a, 0, :], in1=by_sin[:, :, a, 1, :], op=ALU.subtract
                     )
-                    eng.tensor_tensor(
-                        out=res[:, aa, :, HALF:HEAD],
-                        in0=by_sin[:, :, aa, 0, :].rearrange("p m a i -> p a m i"),
-                        in1=by_cos[:, :, aa, 1, :].rearrange("p m a i -> p a m i"),
-                        op=ALU.add,
+                    nc.vector.tensor_tensor(
+                        out=res[:, a, :, HALF:HEAD], in0=by_sin[:, :, a, 0, :], in1=by_cos[:, :, a, 1, :], op=ALU.add
                     )
-                    for a in range(aa.start, aa.stop):
-                        nc.sync.dma_start(out=views[a][:, f * hm : (f + 1) * hm, :], in_=res[:, a])
+                    nc.sync.dma_start(out=views[a][:, f * hm : (f + 1) * hm, :], in_=res[:, a])
 
         keep_warm(WARM_BEFORE)
         for m in range(TOKEN_TILES):

@@ -26,8 +26,8 @@ N_TILE = 512
 LOADS = ((0, 512), (2560, 640), (512, 1024), (1536, 1024))
 GROUPS = ((0, 512, 0), (2560, 640, 1), (512, 1024, 2), (1536, 1024, 3))
 SCALAR_PLANES = ((2, 2), (1, 0), (1, 1), (0, 0))
-UNITS = (((0, 512),), ((0, 512), (512, 128)), ((0, 512), (512, 512)), ((0, 512), (512, 256), (768, 256)))
-RES_BUFS = 16
+UNITS = (((0, 512),), ((0, 512), (512, 128)), ((0, 512), (512, 512)), ((0, 512), (512, 512)))
+RES_BUFS = 24
 BANKS = 8
 WARM_BEFORE = 10
 WARM_BETWEEN = 2

from contextlib import ExitStack

import concourse.mybir as mybir
from concourse.masks import make_identity

TOKENS, HIDDEN, EXPAND, HEAD = 1024, 1024, 1536, 128
COLUMNS = 2 * EXPAND + HEAD
FLOPS = 2 * TOKENS * HIDDEN * COLUMNS

F32 = mybir.dt.float32
BF16 = mybir.dt.bfloat16
U32 = mybir.dt.uint32
U8 = mybir.dt.uint8
FP8 = mybir.dt.float8_e4m3fn
FP8X4 = mybir.dt.float8_e4m3fn_x4
ACT = mybir.ActivationFunctionType
ALU = mybir.AluOpType

P = 128
PACK = 4
PASSES = HIDDEN // (P * PACK)
TOKEN_TILES = TOKENS // P
HALF = HEAD // 2
N_TILE = 512

LOADS = ((0, 512), (2560, 640), (512, 1024), (1536, 1024))
GROUPS = ((0, 512, 0), (2560, 640, 1), (512, 1024, 2), (1536, 1024, 3))
SCALAR_PLANES = ((2, 2), (1, 0), (1, 1), (0, 0))
UNITS = (((0, 512),), ((0, 512), (512, 128)), ((0, 512), (512, 512)), ((0, 512), (512, 512)))
RES_BUFS = 24
BANKS = 8
WARM_BEFORE = 10
WARM_BETWEEN = 2
LATE_BYTES = 4096


def tile_gatedattentionunit_pa_kernel(
    tc, hidden_states, sin, cos, W_i_bytes, W_i_scale, q_scale, k_scale, out_0, out_1, out_2, out_3
):
    nc = tc.nc
    with ExitStack() as ctx:
        const = ctx.enter_context(tc.tile_pool(name="const", bufs=1))
        keep = ctx.enter_context(tc.tile_pool(name="keep", bufs=1))
        stage = ctx.enter_context(tc.tile_pool(name="stage", bufs=4))
        outp = ctx.enter_context(tc.tile_pool(name="outp", bufs=RES_BUFS))
        rope = ctx.enter_context(tc.tile_pool(name="rope", bufs=1))
        late = ctx.enter_context(tc.tile_pool(name="late", bufs=1))
        psum = ctx.enter_context(tc.psum_pool(name="psum", bufs=2))

        w_scale = const.tile([P, PASSES, PACK], F32, name="w_scale")
        nc.scalar.dma_start(
            out=w_scale[:], in_=W_i_scale.rearrange("(g p t) o -> p g (t o)", p=P, t=PACK)
        )
        gain_row = const.tile([P, 2, HEAD], BF16, name="gain_row")
        nc.gpsimd.memset(gain_row[:], 0.0)
        nc.scalar.dma_start(out=gain_row[0:1, 0, :], in_=q_scale.unsqueeze(0))
        nc.scalar.dma_start(out=gain_row[0:1, 1, :], in_=k_scale.unsqueeze(0))
        warm = const.tile([P, 2], F32, name="warm")
        nc.vector.memset(warm[:, 0:1], 0.0)
        nc.scalar.activation(out=warm[:, 1:2], in_=warm[:, 0:1], func=ACT.Silu)
        ones = const.tile([P, P], BF16, name="ones")
        nc.vector.memset(ones[:], 1.0)
        ident = const.tile([P, P], F32, name="ident")
        make_identity(nc, ident[:])
        idle_rhs = const.tile([P, N_TILE], BF16, name="idle_rhs")
        nc.vector.memset(idle_rhs[:], 0.0)

        x_view = hidden_states.rearrange("o (p m) k -> p (o m) k", m=TOKEN_TILES)
        w_view = W_i_bytes.rearrange("(g p t) n -> g p t n", p=P, t=PACK)
        x_sb = [keep.tile([P, 2, HIDDEN], BF16, name="x_sb%d" % h) for h in range(TOKEN_TILES // 2)]
        w_bytes = [
            [keep.tile([P, PACK, width], U8, name="w_bytes%d_%d" % (n, g)) for g in range(PASSES)]
            for n, (c0, width) in enumerate(LOADS)
        ]

        def load_w(n, parts):
            c0, width = LOADS[n]
            step = PACK // parts
            for g in range(PASSES):
                for t in range(0, PACK, step):
                    nc.sync.dma_start(
                        out=w_bytes[n][g][:, t : t + step, :], in_=w_view[g][:, t : t + step, c0 : c0 + width]
                    )

        def load_x(h):
            nc.sync.dma_start(out=x_sb[h][:], in_=x_view[:, 2 * h : 2 * h + 2, :])

        load_w(0, 2)
        load_x(0)
        load_x(1)
        load_w(1, 1)
        load_x(2)
        load_x(3)
        for n in range(2, len(LOADS)):
            load_w(n, 1)
        cos_sb = const.tile([P, TOKEN_TILES, HALF], BF16, name="cos_sb")
        sin_sb = const.tile([P, TOKEN_TILES, HALF], BF16, name="sin_sb")
        nc.sync.dma_start(out=cos_sb[:], in_=cos.rearrange("o (p m) i -> p (o m) i", m=TOKEN_TILES))
        nc.sync.dma_start(out=sin_sb[:], in_=sin.rearrange("o (p m) i -> p (o m) i", m=TOKEN_TILES))

        x_codes = [keep.tile([P, 2 * PASSES * P], U32, name="x_codes%d" % h, align_bytes=64) for h in range(TOKEN_TILES // 2)]
        x_scales = [keep.tile([P, 2 * PASSES * P], U8, name="x_scales%d" % h, align_bytes=64) for h in range(TOKEN_TILES // 2)]
        x_grouped = {}

        def turn_x(m):
            h, a = divmod(m, 2)
            words = x_sb[h][:, a, :].bitcast(F32)
            xt = psum.tile([P, PASSES, 2, P], F32, tag="acc", bufs=BANKS)
            for g in range(PASSES):
                for u in range(2):
                    nc.tensor.transpose(
                        xt[:, g, u, :], words[:, 256 * g + u : 256 * (g + 1) : 2], ident[:]
                    )
            if a == 0:
                x_grouped[h] = stage.tile([P, 2, PASSES, P, PACK], BF16, tag="x_grouped", bufs=4, align_bytes=64, name="x_grouped")
            nc.scalar.copy(
                out=x_grouped[h][:, a].bitcast(F32), in_=xt[:].rearrange("p g u r -> p g r u")
            )

        idle_ps = psum.tile([P, N_TILE], F32, tag="acc", bufs=BANKS, name="idle_ps")

        def keep_warm(count):
            for i in range(count):
                nc.tensor.matmul(out=idle_ps[:], lhsT=ones[:], rhs=idle_rhs[:], start=True, stop=True)

        def quantise_x(h):
            nc.vector.quantize_mx(
                out=x_codes[h][:].bitcast(FP8X4),
                scales=x_scales[h][:],
                in_=x_grouped[h][:].rearrange("p a g r t -> p (a g r t)"),
            )

        w_planes = {}

        def widen(n, scalar_share):
            c0, width, ld = GROUPS[n]
            b0 = c0 - LOADS[ld][0]
            for g in range(PASSES):
                if (n, g) not in w_planes:
                    w_planes[(n, g)] = stage.tile([P, PACK, width], BF16, tag="w_planes", bufs=4, align_bytes=64, name="w_planes")
                planes = w_planes[(n, g)]
                for t in range(PACK):
                    codes = w_bytes[ld][g][:, t, b0 : b0 + width].bitcast(FP8)
                    on_scalar = t >= PACK - SCALAR_PLANES[n][g]
                    if on_scalar and scalar_share:
                        nc.scalar.activation(
                            out=planes[:, t, :], in_=codes, func=ACT.Copy, scale=w_scale[:, g, t : t + 1]
                        )
                    if not on_scalar and not scalar_share:
                        nc.vector.tensor_scalar(
                            out=planes[:, t, :],
                            in0=codes,
                            scalar1=w_scale[:, g, t : t + 1],
                            scalar2=None,
                            op0=ALU.mult,
                        )

        def quantise_w(n, off, w, last):
            codes = keep.tile([P, PASSES * w], U32, name="w_codes%d_%d" % (n, off), align_bytes=64)
            scales = keep.tile([P, PASSES * w], U8, name="w_scales%d_%d" % (n, off), align_bytes=64)
            grouped = []
            for g in range(PASSES):
                if last:
                    gr = late.tile([P, w, PACK], BF16, name="last_grouped%d" % g, offset=g * LATE_BYTES, align_bytes=64)
                else:
                    gr = stage.tile([P, w, PACK], BF16, tag="w_grouped", bufs=4, align_bytes=64, name="w_grouped")
                planes = w_planes[(n, g)]
                if w == HEAD:
                    nc.vector.tensor_copy(
                        out=gr[:].rearrange("p (e i) t -> p e i t", e=2),
                        in_=planes[:, :, off : off + w].rearrange("p t (i e) -> p e i t", e=2),
                    )
                else:
                    nc.vector.tensor_copy(
                        out=gr[:].rearrange("p (c i) t -> p c t i", i=4),
                        in_=planes[:, :, off : off + w].rearrange("p t (c i) -> p c t i", i=4),
                    )
                grouped.append(gr)
            for g in range(PASSES):
                nc.vector.quantize_mx(
                    out=codes[:, g * w : (g + 1) * w].bitcast(FP8X4),
                    scales=scales[:, g * w : (g + 1) * w],
                    in_=grouped[g][:].rearrange("p c t -> p (c t)"),
                )
            return codes, scales

        qk_act = rope.tile([P, TOKEN_TILES, HEAD], F32, name="qk_act")
        out_views = [o.rearrange("o (p m) c -> (o m) p c", m=TOKEN_TILES) for o in (out_0, out_1)]

        def product(acc, codes, scales, w, m):
            h, a = divmod(m, 2)
            for g in range(PASSES):
                x0 = (a * PASSES + g) * P
                nc.tensor.matmul_mx(
                    out=acc,
                    lhsT=x_codes[h][:, x0 : x0 + P].bitcast(FP8X4),
                    lhsT_scale=x_scales[h][:, x0 : x0 + P],
                    rhs=codes[:, g * w : (g + 1) * w].bitcast(FP8X4),
                    rhs_scale=scales[:, g * w : (g + 1) * w],
                    start=(g == 0),
                    stop=(g == PASSES - 1),
                )

        def chunk(c, w, codes, scales):
            if c >= 2 * EXPAND:
                for h in range(TOKEN_TILES // 4):
                    acc = psum.tile([P, 4, HEAD], F32, tag="acc", bufs=BANKS)
                    for r in range(4):
                        product(acc[:, r, :], codes, scales, w, 4 * h + r)
                    nc.scalar.activation(out=qk_act[:, 4 * h : 4 * h + 4, :], in_=acc[:], func=ACT.Silu)
                return
            o, d0 = divmod(c, EXPAND)
            for m in range(TOKEN_TILES):
                acc = psum.tile([P, w], F32, tag="acc", bufs=BANKS)
                product(acc[:], codes, scales, w, m)
                res = outp.tile([P, w], F32, tag="res")
                nc.scalar.activation(out=res[:], in_=acc[:], func=ACT.Silu)
                nc.sync.dma_start(out=out_views[o][m][:, d0 : d0 + w], in_=res[:])

        tables = {}

        def tables_to_psum():
            gains = psum.tile([P, 2, HEAD], F32, tag="acc", bufs=BANKS, name="gains")
            for a in range(2):
                nc.tensor.matmul(
                    out=gains[:, a, :],
                    lhsT=ones[:],
                    rhs=gain_row[:, a, :].rearrange("p (i e) -> p e i", e=2),
                    start=True,
                    stop=True,
                )
            tables["gains"] = gains

        def rotate():
            gains = tables["gains"]
            views = [o.rearrange("o (p m) c -> p (o m) c", m=TOKEN_TILES) for o in (out_2, out_3)]
            hm = TOKEN_TILES // 2
            y = [late.tile([P, hm, 2, HEAD], F32, name="y%d" % f, offset=f * LATE_BYTES, align_bytes=64) for f in range(2)]
            for f in range(2):
                nc.vector.tensor_tensor(
                    out=y[f][:],
                    in0=qk_act[:, f * hm : (f + 1) * hm, :].unsqueeze(2).to_broadcast([P, hm, 2, HEAD]),
                    in1=gains[:].unsqueeze(1).to_broadcast([P, hm, 2, HEAD]),
                    op=ALU.mult,
                )
            for f in range(2):
                by = []
                for s, table in enumerate((cos_sb, sin_sb)):
                    pr = rope.tile([P, hm, 2, 2, HALF], F32, name="by%d_%d" % (f, s))
                    nc.vector.tensor_tensor(
                        out=pr[:].rearrange("p m a e i -> p m (a e) i"),
                        in0=y[f][:].rearrange("p m a (e i) -> p m (a e) i", e=2),
                        in1=table[:, f * hm : (f + 1) * hm, :].unsqueeze(2).to_broadcast([P, hm, 4, HALF]),
                        op=ALU.mult,
                    )
                    by.append(pr)
                by_cos, by_sin = by
                res = rope.tile([P, 2, hm, HEAD], F32, name="rot%d" % f)
                for a in range(2):
                    nc.vector.tensor_tensor(
                        out=res[:, a, :, 0:HALF], in0=by_cos[:, :, a, 0, :], in1=by_sin[:, :, a, 1, :], op=ALU.subtract
                    )
                    nc.vector.tensor_tensor(
                        out=res[:, a, :, HALF:HEAD], in0=by_sin[:, :, a, 0, :], in1=by_cos[:, :, a, 1, :], op=ALU.add
                    )
                    nc.sync.dma_start(out=views[a][:, f * hm : (f + 1) * hm, :], in_=res[:, a])

        keep_warm(WARM_BEFORE)
        for m in range(TOKEN_TILES):
            turn_x(m)
            if m % 2 == 1:
                keep_warm(WARM_BETWEEN)
        widen(0, True)
        for n, (c0, width, ld) in enumerate(GROUPS):
            widen(n, False)
            if n + 1 < len(GROUPS):
                widen(n + 1, True)
            for off, w in UNITS[n]:
                codes, scales = quantise_w(n, off, w, n == len(GROUPS) - 1 and off + w == width)
                if n == 0:
                    for h in range(TOKEN_TILES // 2):
                        quantise_x(h)
                chunk(c0 + off, w, codes, scales)
                if n == 2 and off == 0:
                    tables_to_psum()
        rotate()
